import numpy as np
import ml_dtypes


def mxq(x, axis, fmt="e4m3"):
    dtype, down = {"e4m3": (ml_dtypes.float8_e4m3fn, 7), "e5m2": (ml_dtypes.float8_e5m2, 14)}[fmt]
    v = np.moveaxis(np.asarray(x, np.float32).astype(ml_dtypes.bfloat16).astype(np.float64), axis, -1)
    blocks = v.reshape(v.shape[:-1] + (-1, 32))
    amax = np.abs(blocks).max(-1, keepdims=True)
    byte = np.maximum(np.where(amax > 0, np.frexp(amax)[1] - 1 + 127, 0) - down, 1)
    scale = np.exp2(byte - 127.0)
    codes = (blocks / scale).astype(np.float32).astype(dtype).astype(np.float64)
    return np.moveaxis((codes * scale).reshape(v.shape), -1, axis)


WIDE = False


def mx_kscale(k):
    if not WIDE:
        return np.ones(k)
    levels = np.array([10, -10, 5, -5, 0])
    a = np.random.permutation(np.resize(levels, k // 512 * 4)).reshape(k // 512, 4)
    idx = np.arange(k)
    return np.exp2(a[idx // 512, idx % 128 // 32])


BF16 = ml_dtypes.bfloat16


def bf(x):
    return np.asarray(x, np.float32).astype(BF16)


def f64(x):
    return np.asarray(x).astype(np.float64)


B, N, F, D, O = 4, 1024, 512, 128, 512


def setup_inputs():
    s = mx_kscale(F)
    return {"q": bf(np.random.standard_normal((B, N, D)) * 1.4),
            "k": bf(np.random.standard_normal((B, N, D)) * 1.4),
            "x": bf(np.random.standard_normal((B, N, F)) * s),
            "mask": bf(np.random.randint(0, 2, (B, N))),
            "weight": bf(np.random.standard_normal((F, O)) * 2.0 / np.sqrt(F) / s[:, None])}


def reference(q, k, x, mask, weight):
    sim = f64(q) @ f64(k).transpose(0, 2, 1) / np.sqrt(D)
    e = np.exp(sim - sim.max(-1, keepdims=True))
    support = mxq(f64(x), 2, "e4m3") @ mxq(f64(weight), 0, "e4m3")
    agg = mxq(e, 2, "e4m3") @ mxq(support, 1, "e4m3")
    return agg / e.sum(-1, keepdims=True) * f64(mask)[:, :, None]

@@ -1,0 +1,420 @@
+from contextlib import ExitStack
+import math
+
+import concourse.mybir as mybir
+from concourse.masks import make_identity
+
+FP8X4 = mybir.dt.float8_e4m3fn_x4
+BF16 = mybir.dt.bfloat16
+F32 = mybir.dt.float32
+U32 = mybir.dt.uint32
+U8 = mybir.dt.uint8
+AF = mybir.ActivationFunctionType
+ALU = mybir.AluOpType
+AX = mybir.AxisListType
+
+NB, N, F, D, O = 4, 1024, 512, 128, 512
+P = 128
+FLOPS = 2 * NB * (N * N * D + N * F * O + N * N * O)
+
+NT = 32
+IN_PSUM = ("x", "k", "q", "s")
+
+
+def stream_units():
+    units = [("wg",), ("Qw",)]
+    for b in range(4):
+        units += [("x", b, 0), ("x", b, 1), ("x", b, 2), ("x", b, 3), ("Qx", b, 0)]
+        if b < 3:
+            units += [("k", b + 1)]
+        units += [("Qx", b, 1)]
+        if b < 3:
+            units += [("q", b + 1)]
+        units += [("s", b, 0, 0), ("s", b, 0, 1), ("s", b, 0, 2), ("s", b, 0, 3), ("s", b, 1, 0), ("Qs", b, 0)]
+        units += [("s", b, 1, 1), ("s", b, 1, 2), ("s", b, 1, 3), ("Qs", b, 1)]
+    return units
+
+
+def needs(unit):
+    if unit[0] == "s":
+        return [("Qx", unit[1], unit[2]), ("Qw",)]
+    if unit[0] == "Qw":
+        return [("wg",)]
+    if unit[0] == "Qx":
+        return [("x", unit[1], 2 * unit[2]), ("x", unit[1], 2 * unit[2] + 1)]
+    if unit[0] == "Qs":
+        return [("s", unit[1], unit[2], c) for c in range(4)]
+    return []
+
+
+def make_plan(lag, fill):
+    ops = []
+    stream = stream_units()
+    started = set()
+    done = set([("k", 0), ("q", 0)])
+    st = {"pos": 0, "fly": 0, "tile": 0, "quantised": -1, "summed": -1, "step": 0}
+    vq = []
+    sq = []
+
+    def ready(unit):
+        return all(d in done for d in needs(unit))
+
+    def tile_ready():
+        r = st["tile"]
+        return (r < NT and r <= st["quantised"] and r <= st["summed"] and r <= st["step"] - lag
+                and ("Qs", r // 8, 1) in done)
+
+    def next_in_psum():
+        for unit in stream[st["pos"]:]:
+            if unit[0] in IN_PSUM and unit not in started:
+                return unit if ready(unit) else None
+        return None
+
+    def feed():
+        while st["fly"] < 2:
+            unit = next_in_psum()
+            if unit is not None:
+                started.add(unit)
+                ops.append(("P", "prep") + unit)
+            elif len(started) + 18 == len(stream) and tile_ready():
+                ops.append(("G", st["tile"], "prep"))
+                vq.append(st["tile"])
+                st["tile"] += 1
+            else:
+                return
+            st["fly"] += 1
+
+    def vector_unit():
+        while st["pos"] < len(stream) and stream[st["pos"]] in done:
+            st["pos"] += 1
+        if st["pos"] < len(stream):
+            unit = stream[st["pos"]]
+            if unit in sq or not ready(unit):
+                return
+            if unit[0] in IN_PSUM:
+                if unit not in started:
+                    return
+                st["fly"] -= 1
+            ops.append(("U", "V") + unit)
+            done.add(unit)
+        elif st["vtaken"] < len(vq):
+            ops.append(("H", vq[st["vtaken"]], "V"))
+            st["vtaken"] += 1
+            st["fly"] -= 1
+        feed()
+
+    st["vtaken"] = 0
+    st["staken"] = 0
+    ops.append(("P", "prep", "k", 0))
+    ops.append(("P", "prep", "q", 0))
+    ops.append(("U", "V", "k", 0))
+    ops.append(("U", "S", "q", 0))
+    ops += [("A", 0), ("A", 1), ("B", 0)]
+    feed()
+    while st["tile"] < NT or st["staken"] < len(sq) or st["vtaken"] < len(vq):
+        s = st["step"]
+        if s + 1 < NT:
+            ops.append(("B", s + 1))
+        if s < NT:
+            ops.append(("C", s))
+        if s + 2 < NT:
+            ops.append(("A", s + 2))
+        feed()
+        for rep in range(fill[s % len(fill)]):
+            vector_unit()
+        if 0 <= s - 1 < NT:
+            ops.append(("E", s - 1))
+        if s < NT:
+            ops.append(("T", s))
+        if 0 <= s - 1 < NT:
+            ops.append(("F", s - 1))
+            st["quantised"] = s - 1
+        if s % 2 == 1 and s < NT:
+            ops.append(("R", s // 2))
+            st["summed"] = s
+        if st["staken"] < len(sq):
+            item = sq[st["staken"]]
+            st["staken"] += 1
+            if item[0] == "tile":
+                ops.append(("H", item[1], "S"))
+            else:
+                ops.append(("U", "S") + item)
+                done.add(item)
+        if tile_ready():
+            ops.append(("G", st["tile"], "agg"))
+            sq.append(("tile", st["tile"]))
+            st["tile"] += 1
+        else:
+            unit = next_in_psum()
+            if unit is not None:
+                started.add(unit)
+                sq.append(unit)
+                ops.append(("P", "agg") + unit)
+        feed()
+        st["step"] += 1
+    return ops
+
+
+def tile_graphconvolution_wmask_learnadj_pa_t_kernel(tc, q, k, x, mask, weight, out):
+    nc = tc.nc
+    scale = 1.0 / math.sqrt(D)
+    with ExitStack() as ctx:
+        const = ctx.enter_context(tc.tile_pool(name="const", bufs=1))
+        graph = ctx.enter_context(tc.tile_pool(name="graph", bufs=2))
+        work = ctx.enter_context(tc.tile_pool(name="work", bufs=3))
+        small = ctx.enter_context(tc.tile_pool(name="small", bufs=4))
+        late = ctx.enter_context(tc.tile_pool(name="late", bufs=12))
+        outs = ctx.enter_context(tc.tile_pool(name="outs", bufs=8))
+        ps_sim = ctx.enter_context(tc.psum_pool(name="ps_sim", bufs=4))
+        ps_te = ctx.enter_context(tc.psum_pool(name="ps_te", bufs=1))
+        ps_agg = ctx.enter_context(tc.psum_pool(name="ps_agg", bufs=1))
+        ps_prep = ctx.enter_context(tc.psum_pool(name="ps_prep", bufs=2))
+        banks = {"agg": ps_agg, "prep": ps_prep}
+        ctx.enter_context(tc.manual_schedule())
+
+        ident_bf = const.tile([P, P], BF16, name="ident_bf")
+        make_identity(nc, ident_bf[:])
+        ident_f = const.tile([P, P], F32, name="ident_f")
+        make_identity(nc, ident_f[:])
+
+        k_sb, q_sb, x_sb = {}, {}, {}
+
+        def load_qk(b):
+            k_sb[b] = const.tile([P, 8, D], BF16, name="k_sb%d" % b)
+            nc.sync.dma_start(
+                out=k_sb[b][:].rearrange("p (g t) d -> p g t d", g=2),
+                in_=k[b].rearrange("(g p t) d -> p g t d", g=2, p=P, t=4),
+            )
+            q_sb[b] = const.tile([P, 8, D], BF16, name="q_sb%d" % b)
+            nc.sync.dma_start(out=q_sb[b][:], in_=q[b].rearrange("(p i) d -> p i d", i=8))
+
+        def load_x(b):
+            x_sb[b] = const.tile([P, 8 * F], BF16, name="x_sb%d" % b)
+            nc.sync.dma_start(
+                out=x_sb[b][:].rearrange("p (g t f) -> p g t f", g=2, t=4),
+                in_=x[b].rearrange("(g p t) f -> p g t f", g=2, p=P, t=4),
+            )
+
+        load_qk(0)
+        w_raw = const.tile([P, 4, O], BF16, name="w_raw")
+        nc.sync.dma_start(
+            out=w_raw[:].rearrange("w (u e) o -> w u e o", u=2),
+            in_=weight.rearrange("(u w e) o -> w u e o", u=2, w=P, e=2),
+        )
+        load_x(0)
+        mask_sb = const.tile([P, NB, 8], BF16, name="mask_sb")
+        nc.sync.dma_start(out=mask_sb[:], in_=mask.rearrange("b (p i) -> p b i", i=8))
+        for b in range(1, NB):
+            load_qk(b)
+            load_x(b)
+
+        wg = const.tile([P, 4 * O], BF16, name="wg", align_bytes=64)
+        wc = const.tile([P, O], U32, name="wc", align_bytes=64)
+        ws = const.tile([P, O], U8, name="ws", align_bytes=64)
+        mask_f = const.tile([P, NB * 8], F32, name="mask_f")
+
+        qT, kT, xg, xc, xs, sg, sc, ss = {}, {}, {}, {}, {}, {}, {}, {}
+        bank = {}
+        sim, nbias, rsum, e_sb, te, ge, ec, es, agg, scl = {}, {}, {}, {}, {}, {}, {}, {}, {}, {}
+
+        def copy(eng, dst, src):
+            if eng == "V":
+                nc.vector.tensor_copy(out=dst, in_=src)
+            else:
+                nc.scalar.copy(out=dst, in_=src)
+
+        def quantise(codes, scales, values):
+            nc.vector.quantize_mx(out=codes.bitcast(FP8X4), scales=scales, in_=values)
+
+        def unit_tensor(where, unit):
+            kind, b = unit[0], unit[1]
+            if kind == "k" or kind == "q":
+                src = k_sb[b] if kind == "k" else q_sb[b]
+                pt = banks[where].tile([P, 8, P], BF16, name="pt_" + where, tag=where)
+                for j in range(8):
+                    nc.tensor.transpose(pt[:, j, :], src[:, j, :], ident_bf[:])
+            elif kind == "x":
+                words = x_sb[b][:].bitcast(F32)
+                pt = banks[where].tile([P, 2, 2, P], F32, name="pt_" + where, tag=where)
+                for a in range(2):
+                    for u in range(2):
+                        c0 = (2 * unit[2] + a) * 256 + u * 128
+                        nc.tensor.transpose(pt[:, a, u, :], words[:, c0 : c0 + 128], ident_f[:])
+            else:
+                g, c = unit[2], unit[3]
+                pt = banks[where].tile([P, 4, P], F32, name="pt_" + where, tag=where)
+                for t in range(4):
+                    m0 = (4 * g + t) * 128
+                    nc.tensor.matmul_mx(
+                        out=pt[:, t, :],
+                        lhsT=xc[b][:, m0 : m0 + 128].bitcast(FP8X4),
+                        lhsT_scale=xs[b][:, m0 : m0 + 128],
+                        rhs=wc[:, c * 128 : (c + 1) * 128].bitcast(FP8X4),
+                        rhs_scale=ws[:, c * 128 : (c + 1) * 128],
+                        start=True,
+                        stop=True,
+                    )
+            bank[unit] = pt
+
+        def unit_finish(eng, unit):
+            kind = unit[0]
+            if kind == "wg":
+                nc.vector.tensor_copy(
+                    out=wg[:].rearrange("w (o j) -> w o j", j=4), in_=w_raw[:].rearrange("w j o -> w o j")
+                )
+            elif kind == "Qw":
+                quantise(wc[:], ws[:], wg[:])
+            elif kind == "k" or kind == "q":
+                b = unit[1]
+                dst = graph.tile([P, N], BF16, name=kind + "T")
+                copy(eng, dst[:], bank[unit][:].rearrange("d j p -> d (j p)"))
+                if kind == "k":
+                    kT[b] = dst
+                else:
+                    qT[b] = dst
+            elif kind == "x":
+                b, j = unit[1], unit[2]
+                if b not in xg:
+                    xg[b] = graph.tile([P, 8 * 512], BF16, name="xg", align_bytes=64)
+                view = xg[b][:].bitcast(F32).rearrange("w (a p u) -> w a p u", a=8, p=P, u=2)
+                copy(eng, view[:, 2 * j : 2 * j + 2, :, :], bank[unit][:].rearrange("w a u p -> w a p u"))
+            elif kind == "Qx":
+                b, g = unit[1], unit[2]
+                if b not in xc:
+                    xc[b] = graph.tile([P, 1024], U32, name="xc", align_bytes=64)
+                    xs[b] = graph.tile([P, 1024], U8, name="xs", align_bytes=64)
+                quantise(
+                    xc[b][:, g * 512 : (g + 1) * 512],
+                    xs[b][:, g * 512 : (g + 1) * 512],
+                    xg[b][:, g * 2048 : (g + 1) * 2048],
+                )
+            elif kind == "s":
+                b, g, c = unit[1], unit[2], unit[3]
+                if b not in sg:
+                    sg[b] = graph.tile([P, 2 * 4 * O], BF16, name="sg", align_bytes=64)
+                view = sg[b][:].rearrange("p (g o t) -> p g o t", g=2, o=O, t=4)
+                copy(eng, view[:, g, c * 128 : (c + 1) * 128, :], bank[unit][:].rearrange("p t o -> p o t"))
+            else:
+                b, g = unit[1], unit[2]
+                if b not in sc:
+                    sc[b] = graph.tile([P, 2 * O], U32, name="sc", align_bytes=64)
+                    ss[b] = graph.tile([P, 2 * O], U8, name="ss", align_bytes=64)
+                quantise(
+                    sc[b][:, g * O : (g + 1) * O],
+                    ss[b][:, g * O : (g + 1) * O],
+                    sg[b][:, g * 4 * O : (g + 1) * 4 * O],
+                )
+
+        def similarity(r):
+            b, i = divmod(r, 8)
+            sim[r] = []
+            for g in range(2):
+                ps = ps_sim.tile([P, 512], F32, name="sim", tag="sim")
+                nc.tensor.matmul(
+                    out=ps[:],
+                    lhsT=qT[b][:, i * 128 : (i + 1) * 128],
+                    rhs=kT[b][:, g * 512 : (g + 1) * 512],
+                    start=True,
+                    stop=True,
+                )
+                sim[r].append(ps)
+
+        def row_max(r):
+            mx = small.tile([P, 2], F32, name="mx")
+            for g in range(2):
+                nc.vector.tensor_reduce(out=mx[:, g : g + 1], in_=sim[r][g][:], axis=AX.X, op=ALU.max)
+            nbias[r] = small.tile([P, 1], F32, name="nbias")
+            nc.vector.tensor_scalar(
+                out=nbias[r][:], in0=mx[:, 0:1], scalar1=mx[:, 1:2], scalar2=-scale, op0=ALU.max, op1=ALU.mult
+            )
+
+        def exponential(r):
+            e_sb[r] = work.tile([P, N], BF16, name="e_sb")
+            if r % 2 == 0:
+                rsum[r // 2] = small.tile([P, 2, 2], F32, name="rsum")
+            for g in range(2):
+                nc.scalar.activation(
+                    out=e_sb[r][:, g * 512 : (g + 1) * 512],
+                    in_=sim[r][g][:],
+                    func=AF.Exp,
+                    bias=nbias[r][:, 0:1],
+                    scale=scale,
+                    accum_out=rsum[r // 2][:, r % 2, g : g + 1],
+                )
+
+        def flip(r):
+            te[r] = ps_te.tile([P, 8, P], BF16, name="te", tag="te")
+            for j in range(8):
+                nc.tensor.transpose(te[r][:, j, :], e_sb[r][:, j * 128 : (j + 1) * 128], ident_bf[:])
+
+        def regroup(r):
+            ge[r] = work.tile([P, N], BF16, name="ge", align_bytes=64)
+            copy(
+                "S",
+                ge[r][:].rearrange("p (g n t) -> p g n t", g=2, n=P, t=4),
+                te[r][:].rearrange("p (g t) n -> p g n t", g=2, t=4),
+            )
+
+        def quantise_e(r):
+            ec[r] = late.tile([P, 256], U32, name="ec", align_bytes=64)
+            es[r] = late.tile([P, 256], U8, name="es", align_bytes=64)
+            quantise(ec[r][:], es[r][:], ge[r][:])
+
+        def aggregate(r, where):
+            b = r // 8
+            agg[r] = banks[where].tile([P, O], F32, name="pt_" + where, tag=where)
+            for g in range(2):
+                nc.tensor.matmul_mx(
+                    out=agg[r][:],
+                    lhsT=ec[r][:, g * 128 : (g + 1) * 128].bitcast(FP8X4),
+                    lhsT_scale=es[r][:, g * 128 : (g + 1) * 128],
+                    rhs=sc[b][:, g * O : (g + 1) * O].bitcast(FP8X4),
+                    rhs_scale=ss[b][:, g * O : (g + 1) * O],
+                    start=(g == 0),
+                    stop=(g == 1),
+                )
+
+        def row_scale(pair):
+            if pair == 0:
+                nc.vector.tensor_copy(out=mask_f[:], in_=mask_sb[:].rearrange("p b i -> p (b i)"))
+            total = small.tile([P, 2], F32, name="total")
+            nc.vector.tensor_reduce(out=total[:], in_=rsum[pair][:], axis=AX.X, op=ALU.add)
+            recip = small.tile([P, 2], F32, name="recip")
+            nc.vector.reciprocal(out=recip[:], in_=total[:])
+            scl[pair] = late.tile([P, 2], F32, name="scl")
+            nc.vector.tensor_mul(out=scl[pair][:], in0=recip[:], in1=mask_f[:, 2 * pair : 2 * pair + 2])
+
+        def way_out(r, eng):
+            b, i = divmod(r, 8)
+            o_sb = outs.tile([P, O], F32, name="o_sb")
+            factor = scl[r // 2][:, r % 2 : r % 2 + 1]
+            if eng == "V":
+                nc.vector.tensor_scalar(out=o_sb[:], in0=agg[r][:], scalar1=factor, scalar2=None, op0=ALU.mult)
+            else:
+                nc.scalar.activation(out=o_sb[:], in_=agg[r][:], func=AF.Copy, scale=factor)
+            nc.sync.dma_start(out=out[b].rearrange("(p i) o -> p i o", i=8)[:, i, :], in_=o_sb[:])
+
+        for op in make_plan(1, (2, 2, 2, 3)):
+            what = op[0]
+            if what == "P":
+                unit_tensor(op[1], op[2:])
+            elif what == "U":
+                unit_finish(op[1], op[2:])
+            elif what == "A":
+                similarity(op[1])
+            elif what == "B":
+                row_max(op[1])
+            elif what == "C":
+                exponential(op[1])
+            elif what == "T":
+                flip(op[1])
+            elif what == "E":
+                regroup(op[1])
+            elif what == "F":
+                quantise_e(op[1])
+            elif what == "G":
+                aggregate(op[1], op[2])
+            elif what == "R":
+                row_scale(op[1])
+            else:
+                way_out(op[1], op[2])

@@ -16,6 +16,8 @@ AX = mybir.AxisListType
 NB, N, F, D, O = 4, 1024, 512, 128, 512
 P = 128
 FLOPS = 2 * NB * (N * N * D + N * F * O + N * N * O)
+V_BANKS = 5
+S_BANKS = 3
 
 NT = 32
 IN_PSUM = ("x", "k", "q", "s")
@@ -47,111 +49,140 @@ def needs(unit):
     return []
 
 
-def make_plan(lag, fill):
-    ops = []
+def step_lists(v_extra, s_prep_every, head, late):
     stream = stream_units()
-    started = set()
-    done = set([("k", 0), ("q", 0)])
-    st = {"pos": 0, "fly": 0, "tile": 0, "quantised": -1, "summed": -1, "step": 0}
-    vq = []
-    sq = []
+    when = {("k", 0): -1, ("q", 0): -1}
+    taken = set()
+    st = {"tile": 0, "quantised": -1, "s_count": 0}
+    f_step = {}
+    steps = []
 
-    def ready(unit):
-        return all(d in done for d in needs(unit))
-
-    def tile_ready():
-        r = st["tile"]
-        return (r < NT and r <= st["quantised"] and r <= st["summed"] and r <= st["step"] - lag
-                and ("Qs", r // 8, 1) in done)
-
-    def next_in_psum():
-        for unit in stream[st["pos"]:]:
-            if unit[0] in IN_PSUM and unit not in started:
-                return unit if ready(unit) else None
+    def unit_for(s):
+        for unit in stream:
+            if unit[0] in IN_PSUM and unit not in taken:
+                if all(when.get(d, s) < s for d in needs(unit)):
+                    return unit
+                return None
         return None
 
-    def feed():
-        while st["fly"] < 2:
-            unit = next_in_psum()
-            if unit is not None:
-                started.add(unit)
-                ops.append(("P", "prep") + unit)
-            elif len(started) + 18 == len(stream) and tile_ready():
-                ops.append(("G", st["tile"], "prep"))
-                vq.append(st["tile"])
-                st["tile"] += 1
-            else:
-                return
-            st["fly"] += 1
+    def tile_for(s):
+        r = st["tile"]
+        if r < NT and f_step.get(r, s) < s and when.get(("Qs", r // 8, 1), s) < s and r + 2 < s:
+            return r
+        return None
 
-    def vector_unit():
-        while st["pos"] < len(stream) and stream[st["pos"]] in done:
-            st["pos"] += 1
-        if st["pos"] < len(stream):
-            unit = stream[st["pos"]]
-            if unit in sq or not ready(unit):
-                return
-            if unit[0] in IN_PSUM:
-                if unit not in started:
-                    return
-                st["fly"] -= 1
-            ops.append(("U", "V") + unit)
-            done.add(unit)
-        elif st["vtaken"] < len(vq):
-            ops.append(("H", vq[st["vtaken"]], "V"))
-            st["vtaken"] += 1
-            st["fly"] -= 1
-        feed()
-
-    st["vtaken"] = 0
-    st["staken"] = 0
-    ops.append(("P", "prep", "k", 0))
-    ops.append(("P", "prep", "q", 0))
-    ops.append(("U", "V", "k", 0))
-    ops.append(("U", "S", "q", 0))
-    ops += [("A", 0), ("A", 1), ("B", 0)]
-    feed()
-    while st["tile"] < NT or st["staken"] < len(sq) or st["vtaken"] < len(vq):
-        s = st["step"]
-        if s + 1 < NT:
-            ops.append(("B", s + 1))
-        if s < NT:
-            ops.append(("C", s))
-        if s + 2 < NT:
-            ops.append(("A", s + 2))
-        feed()
-        for rep in range(fill[s % len(fill)]):
-            vector_unit()
-        if 0 <= s - 1 < NT:
-            ops.append(("E", s - 1))
-        if s < NT:
-            ops.append(("T", s))
-        if 0 <= s - 1 < NT:
-            ops.append(("F", s - 1))
-            st["quantised"] = s - 1
-        if s % 2 == 1 and s < NT:
-            ops.append(("R", s // 2))
-            st["summed"] = s
-        if st["staken"] < len(sq):
-            item = sq[st["staken"]]
-            st["staken"] += 1
-            if item[0] == "tile":
-                ops.append(("H", item[1], "S"))
-            else:
-                ops.append(("U", "S") + item)
-                done.add(item)
-        if tile_ready():
-            ops.append(("G", st["tile"], "agg"))
-            sq.append(("tile", st["tile"]))
+    def extra(s, tiles_first):
+        unit, r = unit_for(s), tile_for(s)
+        if r is not None and (tiles_first or unit is None):
             st["tile"] += 1
-        else:
-            unit = next_in_psum()
-            if unit is not None:
-                started.add(unit)
-                sq.append(unit)
-                ops.append(("P", "agg") + unit)
-        feed()
-        st["step"] += 1
+            return ("H", r)
+        if unit is not None:
+            taken.add(unit)
+            when[unit] = s
+            return ("U",) + unit
+        return None
+
+    s = 0
+    while st["tile"] < NT:
+        v, sc = [], []
+        if s < NT:
+            v += [("B", s, 0), ("B", s, 1)]
+        if 0 <= s - 1 < NT:
+            sc.append(("C", s - 1))
+        n_s = head[s] if s < len(head) else (0 if late <= s < NT else 1)
+        for rep in range(n_s):
+            st["s_count"] += 1
+            item = extra(s, st["s_count"] % s_prep_every != 0)
+            if item is not None:
+                sc.append(item)
+        if s == 0:
+            taken.add(("wg",))
+            when[("wg",)] = s
+            sc.append(("U", "wg"))
+        if 0 <= s - 2 < NT:
+            sc.append(("E", s - 2))
+        for rep in range(0 if s == 0 else (3 if s >= late else v_extra[s % len(v_extra)])):
+            item = extra(s, False)
+            if item is not None:
+                v.append(item)
+        if 0 <= s - 3 < NT:
+            v.append(("F", s - 3))
+            f_step[s - 3] = s
+        if s % 2 == 0 and 0 <= s - 2 < NT:
+            v.append(("R", (s - 2) // 2))
+        for unit in stream:
+            if unit[0] not in IN_PSUM and unit not in taken:
+                if all(when.get(d, s) < s or ("U",) + d in v for d in needs(unit)):
+                    taken.add(unit)
+                    when[unit] = s
+                    v.append(("U",) + unit)
+                else:
+                    break
+        steps.append((v, sc))
+        s += 1
+        assert s < 60
+    return steps
+
+
+def fill_of(op):
+    if op[0] == "B":
+        return ("A", op[1], op[2])
+    if op[0] == "E":
+        return ("T", op[1])
+    if op[0] == "H":
+        return ("G", op[1])
+    if op[0] == "U" and op[1] in IN_PSUM:
+        return ("P",) + op[1:]
+    return None
+
+
+def fill_needs(fill):
+    if fill[0] == "A":
+        return [("U", "k", fill[1] // 8), ("U", "q", fill[1] // 8)]
+    if fill[0] == "T":
+        return [("C", fill[1])]
+    if fill[0] == "G":
+        return [("F", fill[1]), ("U", "Qs", fill[1] // 8, 0), ("U", "Qs", fill[1] // 8, 1)]
+    return [("U",) + d for d in needs(fill[1:])]
+
+
+def make_plan(v_banks, s_banks, v_extra, s_prep_every, head, late):
+    steps = [([("U", "k", 0)], [("U", "q", 0)])] + step_lists(v_extra, s_prep_every, head, late)
+    rings = {}
+    for eng, idx, banks in (("V", 0, v_banks), ("S", 1, s_banks)):
+        fills = [fill_of(op) for step in steps for op in step[idx] if fill_of(op) is not None]
+        rings[eng] = {"fills": fills, "banks": banks, "filled": 0, "emptied": 0}
+    ops = []
+    written = set()
+
+    def top_up():
+        progress = True
+        while progress:
+            progress = False
+            for eng in ("S", "V"):
+                ring = rings[eng]
+                if ring["filled"] < len(ring["fills"]) and ring["filled"] - ring["emptied"] < ring["banks"]:
+                    fill = ring["fills"][ring["filled"]]
+                    if all(d in written for d in fill_needs(fill)):
+                        ops.append(fill + (eng,))
+                        ring["filled"] += 1
+                        progress = True
+
+    def write(op, eng):
+        if fill_of(op) is not None:
+            assert rings[eng]["emptied"] < rings[eng]["filled"], op
+            rings[eng]["emptied"] += 1
+        ops.append(op + (eng,))
+        written.add(op)
+        top_up()
+
+    top_up()
+    for v, sc in steps:
+        for i in range(max(len(v), len(sc))):
+            if i < len(v):
+                write(v[i], "V")
+            if i < len(sc):
+                write(sc[i], "S")
     return ops
 
 
@@ -161,15 +192,14 @@ def tile_graphconvolution_wmask_learnadj_pa_t_kernel(tc, q, k, x, mask, weight, 
     with ExitStack() as ctx:
         const = ctx.enter_context(tc.tile_pool(name="const", bufs=1))
         graph = ctx.enter_context(tc.tile_pool(name="graph", bufs=2))
+        graph3 = ctx.enter_context(tc.tile_pool(name="graph3", bufs=3))
         work = ctx.enter_context(tc.tile_pool(name="work", bufs=3))
         small = ctx.enter_context(tc.tile_pool(name="small", bufs=4))
-        late = ctx.enter_context(tc.tile_pool(name="late", bufs=12))
+        late = ctx.enter_context(tc.tile_pool(name="late", bufs=16))
         outs = ctx.enter_context(tc.tile_pool(name="outs", bufs=8))
-        ps_sim = ctx.enter_context(tc.psum_pool(name="ps_sim", bufs=4))
-        ps_te = ctx.enter_context(tc.psum_pool(name="ps_te", bufs=1))
-        ps_agg = ctx.enter_context(tc.psum_pool(name="ps_agg", bufs=1))
-        ps_prep = ctx.enter_context(tc.psum_pool(name="ps_prep", bufs=2))
-        banks = {"agg": ps_agg, "prep": ps_prep}
+        ring_v = ctx.enter_context(tc.psum_pool(name="ring_v", bufs=V_BANKS))
+        ring_s = ctx.enter_context(tc.psum_pool(name="ring_s", bufs=S_BANKS))
+        rings = {"V": ring_v, "S": ring_s}
         ctx.enter_context(tc.manual_schedule())
 
         ident_bf = const.tile([P, P], BF16, name="ident_bf")
@@ -190,18 +220,19 @@ def tile_graphconvolution_wmask_learnadj_pa_t_kernel(tc, q, k, x, mask, weight, 
 
         def load_x(b):
             x_sb[b] = const.tile([P, 8 * F], BF16, name="x_sb%d" % b)
-            nc.sync.dma_start(
-                out=x_sb[b][:].rearrange("p (g t f) -> p g t f", g=2, t=4),
-                in_=x[b].rearrange("(g p t) f -> p g t f", g=2, p=P, t=4),
-            )
+            rows = x[b].rearrange("(g p t) f -> g p t f", g=2, p=P, t=4)
+            for g in range(2):
+                nc.sync.dma_start(
+                    out=x_sb[b][:, g * 4 * F : (g + 1) * 4 * F].rearrange("p (t f) -> p t f", t=4), in_=rows[g]
+                )
 
         load_qk(0)
+        load_x(0)
         w_raw = const.tile([P, 4, O], BF16, name="w_raw")
         nc.sync.dma_start(
             out=w_raw[:].rearrange("w (u e) o -> w u e o", u=2),
             in_=weight.rearrange("(u w e) o -> w u e o", u=2, w=P, e=2),
         )
-        load_x(0)
         mask_sb = const.tile([P, NB, 8], BF16, name="mask_sb")
         nc.sync.dma_start(out=mask_sb[:], in_=mask.rearrange("b (p i) -> p b i", i=8))
         for b in range(1, NB):
@@ -215,7 +246,7 @@ def tile_graphconvolution_wmask_learnadj_pa_t_kernel(tc, q, k, x, mask, weight, 
 
         qT, kT, xg, xc, xs, sg, sc, ss = {}, {}, {}, {}, {}, {}, {}, {}
         bank = {}
-        sim, nbias, rsum, e_sb, te, ge, ec, es, agg, scl = {}, {}, {}, {}, {}, {}, {}, {}, {}, {}
+        sim, half_min, ns, nbias, rsum, e_sb, te, ge, ec, es, agg, scl = {}, {}, {}, {}, {}, {}, {}, {}, {}, {}, {}, {}
 
         def copy(eng, dst, src):
             if eng == "V":
@@ -226,23 +257,23 @@ def tile_graphconvolution_wmask_learnadj_pa_t_kernel(tc, q, k, x, mask, weight, 
         def quantise(codes, scales, values):
             nc.vector.quantize_mx(out=codes.bitcast(FP8X4), scales=scales, in_=values)
 
-        def unit_tensor(where, unit):
+        def unit_tensor(unit, eng):
             kind, b = unit[0], unit[1]
             if kind == "k" or kind == "q":
                 src = k_sb[b] if kind == "k" else q_sb[b]
-                pt = banks[where].tile([P, 8, P], BF16, name="pt_" + where, tag=where)
+                pt = rings[eng].tile([P, 8, P], BF16, name="bank" + eng, tag="bank" + eng)
                 for j in range(8):
                     nc.tensor.transpose(pt[:, j, :], src[:, j, :], ident_bf[:])
             elif kind == "x":
                 words = x_sb[b][:].bitcast(F32)
-                pt = banks[where].tile([P, 2, 2, P], F32, name="pt_" + where, tag=where)
+                pt = rings[eng].tile([P, 2, 2, P], F32, name="bank" + eng, tag="bank" + eng)
                 for a in range(2):
                     for u in range(2):
                         c0 = (2 * unit[2] + a) * 256 + u * 128
                         nc.tensor.transpose(pt[:, a, u, :], words[:, c0 : c0 + 128], ident_f[:])
             else:
                 g, c = unit[2], unit[3]
-                pt = banks[where].tile([P, 4, P], F32, name="pt_" + where, tag=where)
+                pt = rings[eng].tile([P, 4, P], F32, name="bank" + eng, tag="bank" + eng)
                 for t in range(4):
                     m0 = (4 * g + t) * 128
                     nc.tensor.matmul_mx(
@@ -256,12 +287,10 @@ def tile_graphconvolution_wmask_learnadj_pa_t_kernel(tc, q, k, x, mask, weight, 
                     )
             bank[unit] = pt
 
-        def unit_finish(eng, unit):
+        def unit_finish(unit, eng):
             kind = unit[0]
             if kind == "wg":
-                nc.vector.tensor_copy(
-                    out=wg[:].rearrange("w (o j) -> w o j", j=4), in_=w_raw[:].rearrange("w j o -> w o j")
-                )
+                copy(eng, wg[:].rearrange("w (o j) -> w o j", j=4), w_raw[:].rearrange("w j o -> w o j"))
             elif kind == "Qw":
                 quantise(wc[:], ws[:], wg[:])
             elif kind == "k" or kind == "q":
@@ -297,60 +326,62 @@ def tile_graphconvolution_wmask_learnadj_pa_t_kernel(tc, q, k, x, mask, weight, 
             else:
                 b, g = unit[1], unit[2]
                 if b not in sc:
-                    sc[b] = graph.tile([P, 2 * O], U32, name="sc", align_bytes=64)
-                    ss[b] = graph.tile([P, 2 * O], U8, name="ss", align_bytes=64)
+                    sc[b] = graph3.tile([P, 2 * O], U32, name="sc", align_bytes=64)
+                    ss[b] = graph3.tile([P, 2 * O], U8, name="ss", align_bytes=64)
                 quantise(
                     sc[b][:, g * O : (g + 1) * O],
                     ss[b][:, g * O : (g + 1) * O],
                     sg[b][:, g * 4 * O : (g + 1) * 4 * O],
                 )
 
-        def similarity(r):
+        def similarity(r, g, eng):
             b, i = divmod(r, 8)
-            sim[r] = []
-            for g in range(2):
-                ps = ps_sim.tile([P, 512], F32, name="sim", tag="sim")
-                nc.tensor.matmul(
-                    out=ps[:],
-                    lhsT=qT[b][:, i * 128 : (i + 1) * 128],
-                    rhs=kT[b][:, g * 512 : (g + 1) * 512],
-                    start=True,
-                    stop=True,
-                )
-                sim[r].append(ps)
+            sim[(r, g)] = rings[eng].tile([P, 512], F32, name="bank" + eng, tag="bank" + eng)
+            nc.tensor.matmul(
+                out=sim[(r, g)][:],
+                lhsT=qT[b][:, i * 128 : (i + 1) * 128],
+                rhs=kT[b][:, g * 512 : (g + 1) * 512],
+                start=True,
+                stop=True,
+            )
 
-        def row_max(r):
-            mx = small.tile([P, 2], F32, name="mx")
-            for g in range(2):
-                nc.vector.tensor_reduce(out=mx[:, g : g + 1], in_=sim[r][g][:], axis=AX.X, op=ALU.max)
-            nbias[r] = small.tile([P, 1], F32, name="nbias")
+        def row_max(r, g):
+            if g == 0:
+                ns[r] = work.tile([P, N], F32, name="ns", bufs=4)
+                half_min[r] = small.tile([P, 1], F32, name="half_min")
+                nbias[r] = small.tile([P, 1], F32, name="nbias")
             nc.vector.tensor_scalar(
-                out=nbias[r][:], in0=mx[:, 0:1], scalar1=mx[:, 1:2], scalar2=-scale, op0=ALU.max, op1=ALU.mult
+                out=ns[r][:, g * 512 : (g + 1) * 512],
+                in0=sim[(r, g)][:],
+                scalar1=-scale,
+                scalar2=None if g == 0 else half_min[r][:, 0:1],
+                op0=ALU.mult,
+                op1=ALU.min,
+                accum_out=half_min[r][:, 0:1] if g == 0 else nbias[r][:, 0:1],
             )
 
         def exponential(r):
             e_sb[r] = work.tile([P, N], BF16, name="e_sb")
             if r % 2 == 0:
-                rsum[r // 2] = small.tile([P, 2, 2], F32, name="rsum")
-            for g in range(2):
-                nc.scalar.activation(
-                    out=e_sb[r][:, g * 512 : (g + 1) * 512],
-                    in_=sim[r][g][:],
-                    func=AF.Exp,
-                    bias=nbias[r][:, 0:1],
-                    scale=scale,
-                    accum_out=rsum[r // 2][:, r % 2, g : g + 1],
-                )
+                rsum[r // 2] = small.tile([P, 2], F32, name="rsum")
+            nc.scalar.activation(
+                out=e_sb[r][:],
+                in_=ns[r][:],
+                func=AF.Exp,
+                bias=nbias[r][:, 0:1],
+                scale=-1.0,
+                accum_out=rsum[r // 2][:, r % 2 : r % 2 + 1],
+            )
 
-        def flip(r):
-            te[r] = ps_te.tile([P, 8, P], BF16, name="te", tag="te")
+        def flip(r, eng):
+            te[r] = rings[eng].tile([P, 8, P], BF16, name="bank" + eng, tag="bank" + eng)
             for j in range(8):
                 nc.tensor.transpose(te[r][:, j, :], e_sb[r][:, j * 128 : (j + 1) * 128], ident_bf[:])
 
-        def regroup(r):
+        def regroup(r, eng):
             ge[r] = work.tile([P, N], BF16, name="ge", align_bytes=64)
             copy(
-                "S",
+                eng,
                 ge[r][:].rearrange("p (g n t) -> p g n t", g=2, n=P, t=4),
                 te[r][:].rearrange("p (g t) n -> p g n t", g=2, t=4),
             )
@@ -360,9 +391,9 @@ def tile_graphconvolution_wmask_learnadj_pa_t_kernel(tc, q, k, x, mask, weight, 
             es[r] = late.tile([P, 256], U8, name="es", align_bytes=64)
             quantise(ec[r][:], es[r][:], ge[r][:])
 
-        def aggregate(r, where):
+        def aggregate(r, eng):
             b = r // 8
-            agg[r] = banks[where].tile([P, O], F32, name="pt_" + where, tag=where)
+            agg[r] = rings[eng].tile([P, O], F32, name="bank" + eng, tag="bank" + eng)
             for g in range(2):
                 nc.tensor.matmul_mx(
                     out=agg[r][:],
@@ -377,10 +408,8 @@ def tile_graphconvolution_wmask_learnadj_pa_t_kernel(tc, q, k, x, mask, weight, 
         def row_scale(pair):
             if pair == 0:
                 nc.vector.tensor_copy(out=mask_f[:], in_=mask_sb[:].rearrange("p b i -> p (b i)"))
-            total = small.tile([P, 2], F32, name="total")
-            nc.vector.tensor_reduce(out=total[:], in_=rsum[pair][:], axis=AX.X, op=ALU.add)
             recip = small.tile([P, 2], F32, name="recip")
-            nc.vector.reciprocal(out=recip[:], in_=total[:])
+            nc.vector.reciprocal(out=recip[:], in_=rsum[pair][:])
             scl[pair] = late.tile([P, 2], F32, name="scl")
             nc.vector.tensor_mul(out=scl[pair][:], in0=recip[:], in1=mask_f[:, 2 * pair : 2 * pair + 2])
 
@@ -394,27 +423,27 @@ def tile_graphconvolution_wmask_learnadj_pa_t_kernel(tc, q, k, x, mask, weight, 
                 nc.scalar.activation(out=o_sb[:], in_=agg[r][:], func=AF.Copy, scale=factor)
             nc.sync.dma_start(out=out[b].rearrange("(p i) o -> p i o", i=8)[:, i, :], in_=o_sb[:])
 
-        for op in make_plan(1, (2, 2, 2, 3)):
-            what = op[0]
+        for op in make_plan(V_BANKS, S_BANKS, (2, 2, 1), 100, (3, 2, 2), 28):
+            what, eng = op[0], op[-1]
             if what == "P":
-                unit_tensor(op[1], op[2:])
+                unit_tensor(op[1:-1], eng)
             elif what == "U":
-                unit_finish(op[1], op[2:])
+                unit_finish(op[1:-1], eng)
             elif what == "A":
-                similarity(op[1])
+                similarity(op[1], op[2], eng)
             elif what == "B":
-                row_max(op[1])
+                row_max(op[1], op[2])
             elif what == "C":
                 exponential(op[1])
             elif what == "T":
-                flip(op[1])
+                flip(op[1], eng)
             elif what == "E":
-                regroup(op[1])
+                regroup(op[1], eng)
             elif what == "F":
                 quantise_e(op[1])
             elif what == "G":
-                aggregate(op[1], op[2])
+                aggregate(op[1], eng)
             elif what == "R":
                 row_scale(op[1])
             else:
-                way_out(op[1], op[2])
+                way_out(op[1], eng)

@@ -49,7 +49,7 @@ def needs(unit):
     return []
 
 
-def step_lists(v_extra, s_prep_every, head, late):
+def step_lists(v_extra, s_extra, head, late, pool):
     stream = stream_units()
     when = {("k", 0): -1, ("q", 0): -1}
     taken = set()
@@ -89,10 +89,9 @@ def step_lists(v_extra, s_prep_every, head, late):
             v += [("B", s, 0), ("B", s, 1)]
         if 0 <= s - 1 < NT:
             sc.append(("C", s - 1))
-        n_s = head[s] if s < len(head) else (0 if late <= s < NT else 1)
+        n_s = head[s] if s < len(head) else (0 if late <= s < NT else s_extra[s % len(s_extra)])
         for rep in range(n_s):
-            st["s_count"] += 1
-            item = extra(s, st["s_count"] % s_prep_every != 0)
+            item = extra(s, True)
             if item is not None:
                 sc.append(item)
         if s == 0:
@@ -101,13 +100,15 @@ def step_lists(v_extra, s_prep_every, head, late):
             sc.append(("U", "wg"))
         if 0 <= s - 2 < NT:
             sc.append(("E", s - 2))
+            if pool:
+                sc.append(("W", s - 2))
         for rep in range(0 if s == 0 else (3 if s >= late else v_extra[s % len(v_extra)])):
             item = extra(s, False)
             if item is not None:
                 v.append(item)
-        if 0 <= s - 3 < NT:
-            v.append(("F", s - 3))
-            f_step[s - 3] = s
+        if 0 <= s - 3 - pool < NT:
+            v.append(("F", s - 3 - pool))
+            f_step[s - 3 - pool] = s
         if s % 2 == 0 and 0 <= s - 2 < NT:
             v.append(("R", (s - 2) // 2))
         for unit in stream:
@@ -146,8 +147,8 @@ def fill_needs(fill):
     return [("U",) + d for d in needs(fill[1:])]
 
 
-def make_plan(v_banks, s_banks, v_extra, s_prep_every, head, late):
-    steps = [([("U", "k", 0)], [("U", "q", 0)])] + step_lists(v_extra, s_prep_every, head, late)
+def make_plan(v_banks, s_banks, v_extra, s_extra, head, late, pool):
+    steps = [([("U", "k", 0)], [("U", "q", 0)])] + step_lists(v_extra, s_extra, head, late, pool)
     rings = {}
     for eng, idx, banks in (("V", 0, v_banks), ("S", 1, s_banks)):
         fills = [fill_of(op) for step in steps for op in step[idx] if fill_of(op) is not None]
@@ -182,7 +183,7 @@ def make_plan(v_banks, s_banks, v_extra, s_prep_every, head, late):
             if i < len(v):
                 write(v[i], "V")
             if i < len(sc):
-                write(sc[i], "S")
+                write(sc[i], "G" if sc[i][0] == "W" else "S")
     return ops
 
 
@@ -195,8 +196,8 @@ def tile_graphconvolution_wmask_learnadj_pa_t_kernel(tc, q, k, x, mask, weight, 
         graph3 = ctx.enter_context(tc.tile_pool(name="graph3", bufs=3))
         work = ctx.enter_context(tc.tile_pool(name="work", bufs=3))
         small = ctx.enter_context(tc.tile_pool(name="small", bufs=4))
-        late = ctx.enter_context(tc.tile_pool(name="late", bufs=16))
-        outs = ctx.enter_context(tc.tile_pool(name="outs", bufs=8))
+        late = ctx.enter_context(tc.tile_pool(name="late", bufs=20))
+        outs = ctx.enter_context(tc.tile_pool(name="outs", bufs=12))
         ring_v = ctx.enter_context(tc.psum_pool(name="ring_v", bufs=V_BANKS))
         ring_s = ctx.enter_context(tc.psum_pool(name="ring_s", bufs=S_BANKS))
         rings = {"V": ring_v, "S": ring_s}
@@ -423,7 +424,7 @@ def tile_graphconvolution_wmask_learnadj_pa_t_kernel(tc, q, k, x, mask, weight, 
                 nc.scalar.activation(out=o_sb[:], in_=agg[r][:], func=AF.Copy, scale=factor)
             nc.sync.dma_start(out=out[b].rearrange("(p i) o -> p i o", i=8)[:, i, :], in_=o_sb[:])
 
-        for op in make_plan(V_BANKS, S_BANKS, (2, 2, 1), 100, (3, 2, 2), 28):
+        for op in make_plan(V_BANKS, S_BANKS, (2, 2, 1), (1, 0), (3, 2, 2), 40, 0):
             what, eng = op[0], op[-1]
             if what == "P":
                 unit_tensor(op[1:-1], eng)

@@ -49,7 +49,7 @@ def needs(unit):
     return []
 
 
-def step_lists(v_extra, s_extra, head, late, pool):
+def step_lists(v_extra, s_prep_every, head, late):
     stream = stream_units()
     when = {("k", 0): -1, ("q", 0): -1}
     taken = set()
@@ -89,9 +89,10 @@ def step_lists(v_extra, s_extra, head, late, pool):
             v += [("B", s, 0), ("B", s, 1)]
         if 0 <= s - 1 < NT:
             sc.append(("C", s - 1))
-        n_s = head[s] if s < len(head) else (0 if late <= s < NT else s_extra[s % len(s_extra)])
+        n_s = head[s] if s < len(head) else (0 if late <= s < NT else 1)
         for rep in range(n_s):
-            item = extra(s, True)
+            st["s_count"] += 1
+            item = extra(s, st["s_count"] % s_prep_every != 0)
             if item is not None:
                 sc.append(item)
         if s == 0:
@@ -100,15 +101,13 @@ def step_lists(v_extra, s_extra, head, late, pool):
             sc.append(("U", "wg"))
         if 0 <= s - 2 < NT:
             sc.append(("E", s - 2))
-            if pool:
-                sc.append(("W", s - 2))
         for rep in range(0 if s == 0 else (3 if s >= late else v_extra[s % len(v_extra)])):
             item = extra(s, False)
             if item is not None:
                 v.append(item)
-        if 0 <= s - 3 - pool < NT:
-            v.append(("F", s - 3 - pool))
-            f_step[s - 3 - pool] = s
+        if 0 <= s - 3 < NT:
+            v.append(("F", s - 3))
+            f_step[s - 3] = s
         if s % 2 == 0 and 0 <= s - 2 < NT:
             v.append(("R", (s - 2) // 2))
         for unit in stream:
@@ -147,8 +146,8 @@ def fill_needs(fill):
     return [("U",) + d for d in needs(fill[1:])]
 
 
-def make_plan(v_banks, s_banks, v_extra, s_extra, head, late, pool):
-    steps = [([("U", "k", 0)], [("U", "q", 0)])] + step_lists(v_extra, s_extra, head, late, pool)
+def make_plan(v_banks, s_banks, v_extra, s_prep_every, head, late):
+    steps = [([("U", "k", 0)], [("U", "q", 0)])] + step_lists(v_extra, s_prep_every, head, late)
     rings = {}
     for eng, idx, banks in (("V", 0, v_banks), ("S", 1, s_banks)):
         fills = [fill_of(op) for step in steps for op in step[idx] if fill_of(op) is not None]
@@ -183,7 +182,7 @@ def make_plan(v_banks, s_banks, v_extra, s_extra, head, late, pool):
             if i < len(v):
                 write(v[i], "V")
             if i < len(sc):
-                write(sc[i], "G" if sc[i][0] == "W" else "S")
+                write(sc[i], "S")
     return ops
 
 
@@ -196,12 +195,11 @@ def tile_graphconvolution_wmask_learnadj_pa_t_kernel(tc, q, k, x, mask, weight, 
         graph3 = ctx.enter_context(tc.tile_pool(name="graph3", bufs=3))
         work = ctx.enter_context(tc.tile_pool(name="work", bufs=3))
         small = ctx.enter_context(tc.tile_pool(name="small", bufs=4))
-        late = ctx.enter_context(tc.tile_pool(name="late", bufs=20))
-        outs = ctx.enter_context(tc.tile_pool(name="outs", bufs=12))
+        late = ctx.enter_context(tc.tile_pool(name="late", bufs=16))
+        outs = ctx.enter_context(tc.tile_pool(name="outs", bufs=8))
         ring_v = ctx.enter_context(tc.psum_pool(name="ring_v", bufs=V_BANKS))
         ring_s = ctx.enter_context(tc.psum_pool(name="ring_s", bufs=S_BANKS))
         rings = {"V": ring_v, "S": ring_s}
-        ctx.enter_context(tc.manual_schedule())
 
         ident_bf = const.tile([P, P], BF16, name="ident_bf")
         make_identity(nc, ident_bf[:])
@@ -424,7 +422,7 @@ def tile_graphconvolution_wmask_learnadj_pa_t_kernel(tc, q, k, x, mask, weight, 
                 nc.scalar.activation(out=o_sb[:], in_=agg[r][:], func=AF.Copy, scale=factor)
             nc.sync.dma_start(out=out[b].rearrange("(p i) o -> p i o", i=8)[:, i, :], in_=o_sb[:])
 
-        for op in make_plan(V_BANKS, S_BANKS, (2, 2, 1), (1, 0), (3, 2, 2), 40, 0):
+        for op in make_plan(V_BANKS, S_BANKS, (2, 2, 1), 100, (3, 2, 2), 28):
             what, eng = op[0], op[-1]
             if what == "P":
                 unit_tensor(op[1:-1], eng)

@@ -18,6 +18,9 @@ P = 128
 FLOPS = 2 * NB * (N * N * D + N * F * O + N * N * O)
 V_BANKS = 5
 S_BANKS = 3
+FG = 2
+RG = 4
+LATE_BUFS = 10
 
 NT = 32
 IN_PSUM = ("x", "k", "q", "s")
@@ -26,35 +29,34 @@ IN_PSUM = ("x", "k", "q", "s")
 def stream_units():
     units = [("wg",), ("Qw",)]
     for b in range(4):
-        units += [("x", b, 0), ("x", b, 1), ("x", b, 2), ("x", b, 3), ("Qx", b, 0)]
+        units += [("x", b, j) for j in range(4)]
         if b < 3:
-            units += [("k", b + 1)]
-        units += [("Qx", b, 1)]
-        if b < 3:
-            units += [("q", b + 1)]
-        units += [("s", b, 0, 0), ("s", b, 0, 1), ("s", b, 0, 2), ("s", b, 0, 3), ("s", b, 1, 0), ("Qs", b, 0)]
-        units += [("s", b, 1, 1), ("s", b, 1, 2), ("s", b, 1, 3), ("Qs", b, 1)]
+            units += [("k", b + 1), ("q", b + 1)]
+        units += [("Qx", b)]
+        units += [("s", b, g, c) for g in range(2) for c in range(4)]
+        units += [("Qs", b)]
     return units
 
 
 def needs(unit):
     if unit[0] == "s":
-        return [("Qx", unit[1], unit[2]), ("Qw",)]
+        return [("Qx", unit[1]), ("Qw",)]
     if unit[0] == "Qw":
         return [("wg",)]
     if unit[0] == "Qx":
-        return [("x", unit[1], 2 * unit[2]), ("x", unit[1], 2 * unit[2] + 1)]
+        return [("x", unit[1], j) for j in range(4)]
     if unit[0] == "Qs":
-        return [("s", unit[1], unit[2], c) for c in range(4)]
+        return [("s", unit[1], g, c) for g in range(2) for c in range(4)]
     return []
 
 
-def step_lists(v_extra, s_prep_every, head, late):
+def step_lists(v_extra, s_extra, head, late, pool, fg, rg):
     stream = stream_units()
     when = {("k", 0): -1, ("q", 0): -1}
     taken = set()
-    st = {"tile": 0, "quantised": -1, "s_count": 0}
+    st = {"tile": 0}
     f_step = {}
+    r_step = {}
     steps = []
 
     def unit_for(s):
@@ -67,7 +69,7 @@ def step_lists(v_extra, s_prep_every, head, late):
 
     def tile_for(s):
         r = st["tile"]
-        if r < NT and f_step.get(r, s) < s and when.get(("Qs", r // 8, 1), s) < s and r + 2 < s:
+        if r < NT and f_step.get(r // fg, s) < s and r_step.get(r // rg, s) < s and when.get(("Qs", r // 8), s) < s:
             return r
         return None
 
@@ -89,10 +91,9 @@ def step_lists(v_extra, s_prep_every, head, late):
             v += [("B", s, 0), ("B", s, 1)]
         if 0 <= s - 1 < NT:
             sc.append(("C", s - 1))
-        n_s = head[s] if s < len(head) else (0 if late <= s < NT else 1)
+        n_s = head[s] if s < len(head) else (0 if late <= s < NT else s_extra[s % len(s_extra)])
         for rep in range(n_s):
-            st["s_count"] += 1
-            item = extra(s, st["s_count"] % s_prep_every != 0)
+            item = extra(s, True)
             if item is not None:
                 sc.append(item)
         if s == 0:
@@ -100,16 +101,23 @@ def step_lists(v_extra, s_prep_every, head, late):
             when[("wg",)] = s
             sc.append(("U", "wg"))
         if 0 <= s - 2 < NT:
-            sc.append(("E", s - 2))
+            if pool:
+                v.append(("E", s - 2))
+                v.append(("W", s - 2))
+            else:
+                sc.append(("E", s - 2))
         for rep in range(0 if s == 0 else (3 if s >= late else v_extra[s % len(v_extra)])):
             item = extra(s, False)
             if item is not None:
                 v.append(item)
-        if 0 <= s - 3 < NT:
-            v.append(("F", s - 3))
-            f_step[s - 3] = s
-        if s % 2 == 0 and 0 <= s - 2 < NT:
-            v.append(("R", (s - 2) // 2))
+        r = s - 3 - pool
+        if 0 <= r < NT and r % fg == fg - 1:
+            v.append(("F", r // fg))
+            f_step[r // fg] = s
+        r = s - 2
+        if 0 <= r < NT and r % rg == rg - 1:
+            v.append(("R", r // rg))
+            r_step[r // rg] = s
         for unit in stream:
             if unit[0] not in IN_PSUM and unit not in taken:
                 if all(when.get(d, s) < s or ("U",) + d in v for d in needs(unit)):
@@ -120,7 +128,7 @@ def step_lists(v_extra, s_prep_every, head, late):
                     break
         steps.append((v, sc))
         s += 1
-        assert s < 60
+        assert s < 70
     return steps
 
 
@@ -136,18 +144,18 @@ def fill_of(op):
     return None
 
 
-def fill_needs(fill):
-    if fill[0] == "A":
-        return [("U", "k", fill[1] // 8), ("U", "q", fill[1] // 8)]
-    if fill[0] == "T":
-        return [("C", fill[1])]
-    if fill[0] == "G":
-        return [("F", fill[1]), ("U", "Qs", fill[1] // 8, 0), ("U", "Qs", fill[1] // 8, 1)]
-    return [("U",) + d for d in needs(fill[1:])]
+def make_plan(v_banks, s_banks, v_extra, s_extra, head, late, pool, fg, rg):
+    steps = [([("U", "k", 0)], [("U", "q", 0)])] + step_lists(v_extra, s_extra, head, late, pool, fg, rg)
 
+    def fill_needs(fill):
+        if fill[0] == "A":
+            return [("U", "k", fill[1] // 8), ("U", "q", fill[1] // 8)]
+        if fill[0] == "T":
+            return [("C", fill[1])]
+        if fill[0] == "G":
+            return [("F", fill[1] // fg), ("U", "Qs", fill[1] // 8)]
+        return [("U",) + d for d in needs(fill[1:])]
 
-def make_plan(v_banks, s_banks, v_extra, s_prep_every, head, late):
-    steps = [([("U", "k", 0)], [("U", "q", 0)])] + step_lists(v_extra, s_prep_every, head, late)
     rings = {}
     for eng, idx, banks in (("V", 0, v_banks), ("S", 1, s_banks)):
         fills = [fill_of(op) for step in steps for op in step[idx] if fill_of(op) is not None]
@@ -180,7 +188,7 @@ def make_plan(v_banks, s_banks, v_extra, s_prep_every, head, late):
     for v, sc in steps:
         for i in range(max(len(v), len(sc))):
             if i < len(v):
-                write(v[i], "V")
+                write(v[i], "G" if v[i][0] == "W" else "V")
             if i < len(sc):
                 write(sc[i], "S")
     return ops
@@ -195,8 +203,8 @@ def tile_graphconvolution_wmask_learnadj_pa_t_kernel(tc, q, k, x, mask, weight, 
         graph3 = ctx.enter_context(tc.tile_pool(name="graph3", bufs=3))
         work = ctx.enter_context(tc.tile_pool(name="work", bufs=3))
         small = ctx.enter_context(tc.tile_pool(name="small", bufs=4))
-        late = ctx.enter_context(tc.tile_pool(name="late", bufs=16))
-        outs = ctx.enter_context(tc.tile_pool(name="outs", bufs=8))
+        late = ctx.enter_context(tc.tile_pool(name="late", bufs=LATE_BUFS))
+        outs = ctx.enter_context(tc.tile_pool(name="outs", bufs=12))
         ring_v = ctx.enter_context(tc.psum_pool(name="ring_v", bufs=V_BANKS))
         ring_s = ctx.enter_context(tc.psum_pool(name="ring_s", bufs=S_BANKS))
         rings = {"V": ring_v, "S": ring_s}
@@ -245,6 +253,7 @@ def tile_graphconvolution_wmask_learnadj_pa_t_kernel(tc, q, k, x, mask, weight, 
 
         qT, kT, xg, xc, xs, sg, sc, ss = {}, {}, {}, {}, {}, {}, {}, {}
         bank = {}
+        planes = {}
         sim, half_min, ns, nbias, rsum, e_sb, te, ge, ec, es, agg, scl = {}, {}, {}, {}, {}, {}, {}, {}, {}, {}, {}, {}
 
         def copy(eng, dst, src):
@@ -307,15 +316,10 @@ def tile_graphconvolution_wmask_learnadj_pa_t_kernel(tc, q, k, x, mask, weight, 
                 view = xg[b][:].bitcast(F32).rearrange("w (a p u) -> w a p u", a=8, p=P, u=2)
                 copy(eng, view[:, 2 * j : 2 * j + 2, :, :], bank[unit][:].rearrange("w a u p -> w a p u"))
             elif kind == "Qx":
-                b, g = unit[1], unit[2]
-                if b not in xc:
-                    xc[b] = graph.tile([P, 1024], U32, name="xc", align_bytes=64)
-                    xs[b] = graph.tile([P, 1024], U8, name="xs", align_bytes=64)
-                quantise(
-                    xc[b][:, g * 512 : (g + 1) * 512],
-                    xs[b][:, g * 512 : (g + 1) * 512],
-                    xg[b][:, g * 2048 : (g + 1) * 2048],
-                )
+                b = unit[1]
+                xc[b] = graph.tile([P, 1024], U32, name="xc", align_bytes=64)
+                xs[b] = graph.tile([P, 1024], U8, name="xs", align_bytes=64)
+                quantise(xc[b][:], xs[b][:], xg[b][:])
             elif kind == "s":
                 b, g, c = unit[1], unit[2], unit[3]
                 if b not in sg:
@@ -323,15 +327,10 @@ def tile_graphconvolution_wmask_learnadj_pa_t_kernel(tc, q, k, x, mask, weight, 
                 view = sg[b][:].rearrange("p (g o t) -> p g o t", g=2, o=O, t=4)
                 copy(eng, view[:, g, c * 128 : (c + 1) * 128, :], bank[unit][:].rearrange("p t o -> p o t"))
             else:
-                b, g = unit[1], unit[2]
-                if b not in sc:
-                    sc[b] = graph3.tile([P, 2 * O], U32, name="sc", align_bytes=64)
-                    ss[b] = graph3.tile([P, 2 * O], U8, name="ss", align_bytes=64)
-                quantise(
-                    sc[b][:, g * O : (g + 1) * O],
-                    ss[b][:, g * O : (g + 1) * O],
-                    sg[b][:, g * 4 * O : (g + 1) * 4 * O],
-                )
+                b = unit[1]
+                sc[b] = graph3.tile([P, 2 * O], U32, name="sc", align_bytes=64)
+                ss[b] = graph3.tile([P, 2 * O], U8, name="ss", align_bytes=64)
+                quantise(sc[b][:], ss[b][:], sg[b][:])
 
         def similarity(r, g, eng):
             b, i = divmod(r, 8)
@@ -361,15 +360,15 @@ def tile_graphconvolution_wmask_learnadj_pa_t_kernel(tc, q, k, x, mask, weight, 
 
         def exponential(r):
             e_sb[r] = work.tile([P, N], BF16, name="e_sb")
-            if r % 2 == 0:
-                rsum[r // 2] = small.tile([P, 2], F32, name="rsum")
+            if r % RG == 0:
+                rsum[r // RG] = small.tile([P, RG], F32, name="rsum")
             nc.scalar.activation(
                 out=e_sb[r][:],
                 in_=ns[r][:],
                 func=AF.Exp,
                 bias=nbias[r][:, 0:1],
                 scale=-1.0,
-                accum_out=rsum[r // 2][:, r % 2 : r % 2 + 1],
+                accum_out=rsum[r // RG][:, r % RG : r % RG + 1],
             )
 
         def flip(r, eng):
@@ -378,26 +377,35 @@ def tile_graphconvolution_wmask_learnadj_pa_t_kernel(tc, q, k, x, mask, weight, 
                 nc.tensor.transpose(te[r][:, j, :], e_sb[r][:, j * 128 : (j + 1) * 128], ident_bf[:])
 
         def regroup(r, eng):
-            ge[r] = work.tile([P, N], BF16, name="ge", align_bytes=64)
-            copy(
-                eng,
-                ge[r][:].rearrange("p (g n t) -> p g n t", g=2, n=P, t=4),
-                te[r][:].rearrange("p (g t) n -> p g n t", g=2, t=4),
+            planes[r] = work.tile([P, N], BF16, name="planes")
+            copy(eng, planes[r][:], te[r][:].rearrange("p j n -> p (j n)"))
+
+        def interleave(r):
+            if r % FG == 0:
+                ge[r // FG] = work.tile([P, FG * N], BF16, name="ge", align_bytes=64)
+            nc.gpsimd.tensor_scalar(
+                out=ge[r // FG][:, (r % FG) * N : (r % FG + 1) * N].rearrange("p (g n t) -> p g n t", g=2, n=P, t=4),
+                in0=planes[r][:].rearrange("p (g t n) -> p g n t", g=2, t=4),
+                scalar1=1.0,
+                scalar2=0.0,
+                op0=ALU.mult,
+                op1=ALU.add,
             )
 
-        def quantise_e(r):
-            ec[r] = late.tile([P, 256], U32, name="ec", align_bytes=64)
-            es[r] = late.tile([P, 256], U8, name="es", align_bytes=64)
-            quantise(ec[r][:], es[r][:], ge[r][:])
+        def quantise_e(f):
+            ec[f] = late.tile([P, FG * 256], U32, name="ec", align_bytes=64)
+            es[f] = late.tile([P, FG * 256], U8, name="es", align_bytes=64)
+            quantise(ec[f][:], es[f][:], ge[f][:])
 
         def aggregate(r, eng):
             b = r // 8
             agg[r] = rings[eng].tile([P, O], F32, name="bank" + eng, tag="bank" + eng)
             for g in range(2):
+                n0 = (r % FG) * 256 + g * 128
                 nc.tensor.matmul_mx(
                     out=agg[r][:],
-                    lhsT=ec[r][:, g * 128 : (g + 1) * 128].bitcast(FP8X4),
-                    lhsT_scale=es[r][:, g * 128 : (g + 1) * 128],
+                    lhsT=ec[r // FG][:, n0 : n0 + 128].bitcast(FP8X4),
+                    lhsT_scale=es[r // FG][:, n0 : n0 + 128],
                     rhs=sc[b][:, g * O : (g + 1) * O].bitcast(FP8X4),
                     rhs_scale=ss[b][:, g * O : (g + 1) * O],
                     start=(g == 0),
@@ -407,22 +415,22 @@ def tile_graphconvolution_wmask_learnadj_pa_t_kernel(tc, q, k, x, mask, weight, 
         def row_scale(pair):
             if pair == 0:
                 nc.vector.tensor_copy(out=mask_f[:], in_=mask_sb[:].rearrange("p b i -> p (b i)"))
-            recip = small.tile([P, 2], F32, name="recip")
+            recip = small.tile([P, RG], F32, name="recip")
             nc.vector.reciprocal(out=recip[:], in_=rsum[pair][:])
-            scl[pair] = late.tile([P, 2], F32, name="scl")
-            nc.vector.tensor_mul(out=scl[pair][:], in0=recip[:], in1=mask_f[:, 2 * pair : 2 * pair + 2])
+            scl[pair] = late.tile([P, RG], F32, name="scl")
+            nc.vector.tensor_mul(out=scl[pair][:], in0=recip[:], in1=mask_f[:, RG * pair : RG * pair + RG])
 
         def way_out(r, eng):
             b, i = divmod(r, 8)
             o_sb = outs.tile([P, O], F32, name="o_sb")
-            factor = scl[r // 2][:, r % 2 : r % 2 + 1]
+            factor = scl[r // RG][:, r % RG : r % RG + 1]
             if eng == "V":
                 nc.vector.tensor_scalar(out=o_sb[:], in0=agg[r][:], scalar1=factor, scalar2=None, op0=ALU.mult)
             else:
                 nc.scalar.activation(out=o_sb[:], in_=agg[r][:], func=AF.Copy, scale=factor)
             nc.sync.dma_start(out=out[b].rearrange("(p i) o -> p i o", i=8)[:, i, :], in_=o_sb[:])
 
-        for op in make_plan(V_BANKS, S_BANKS, (2, 2, 1), 100, (3, 2, 2), 28):
+        for op in make_plan(V_BANKS, S_BANKS, (0, 1), (2,), (3, 3, 3), 40, 1, FG, RG):
             what, eng = op[0], op[-1]
             if what == "P":
                 unit_tensor(op[1:-1], eng)
@@ -438,6 +446,8 @@ def tile_graphconvolution_wmask_learnadj_pa_t_kernel(tc, q, k, x, mask, weight, 
                 flip(op[1], eng)
             elif what == "E":
                 regroup(op[1], eng)
+            elif what == "W":
+                interleave(op[1])
             elif what == "F":
                 quantise_e(op[1])
             elif what == "G":

@@ -23,7 +23,7 @@ RG = 4
 LATE_BUFS = 10
 
 NT = 32
-IN_PSUM = ("x", "k", "q", "s")
+IN_PSUM = ("x", "kq", "s")
 
 
 def stream_units():
@@ -31,7 +31,7 @@ def stream_units():
     for b in range(4):
         units += [("x", b, j) for j in range(4)]
         if b < 3:
-            units += [("k", b + 1), ("q", b + 1)]
+            units += [("kq", b + 1, 0), ("kq", b + 1, 1)]
         units += [("Qx", b)]
         units += [("s", b, g, c) for g in range(2) for c in range(4)]
         units += [("Qs", b)]
@@ -52,7 +52,7 @@ def needs(unit):
 
 def step_lists(v_extra, s_extra, head, late, pool, fg, rg):
     stream = stream_units()
-    when = {("k", 0): -1, ("q", 0): -1}
+    when = {("kq", 0, 0): -1, ("kq", 0, 1): -1}
     taken = set()
     st = {"tile": 0}
     f_step = {}
@@ -145,11 +145,11 @@ def fill_of(op):
 
 
 def make_plan(v_banks, s_banks, v_extra, s_extra, head, late, pool, fg, rg):
-    steps = [([("U", "k", 0)], [("U", "q", 0)])] + step_lists(v_extra, s_extra, head, late, pool, fg, rg)
+    steps = [([("U", "kq", 0, 0)], [("U", "kq", 0, 1)])] + step_lists(v_extra, s_extra, head, late, pool, fg, rg)
 
     def fill_needs(fill):
         if fill[0] == "A":
-            return [("U", "k", fill[1] // 8), ("U", "q", fill[1] // 8)]
+            return [("U", "kq", fill[1] // 8, fill[2]), ("U", "kq", fill[1] // 8, (fill[1] % 8) // 4)]
         if fill[0] == "T":
             return [("C", fill[1])]
         if fill[0] == "G":
@@ -190,7 +190,7 @@ def make_plan(v_banks, s_banks, v_extra, s_extra, head, late, pool, fg, rg):
             if i < len(v):
                 write(v[i], "G" if v[i][0] == "W" else "V")
             if i < len(sc):
-                write(sc[i], "S")
+                write(sc[i], "G" if sc[i] == ("U", "wg") else "S")
     return ops
 
 
@@ -218,12 +218,12 @@ def tile_graphconvolution_wmask_learnadj_pa_t_kernel(tc, q, k, x, mask, weight, 
 
         def load_qk(b):
             k_sb[b] = const.tile([P, 8, D], BF16, name="k_sb%d" % b)
-            nc.sync.dma_start(
-                out=k_sb[b][:].rearrange("p (g t) d -> p g t d", g=2),
-                in_=k[b].rearrange("(g p t) d -> p g t d", g=2, p=P, t=4),
-            )
             q_sb[b] = const.tile([P, 8, D], BF16, name="q_sb%d" % b)
-            nc.sync.dma_start(out=q_sb[b][:], in_=q[b].rearrange("(p i) d -> p i d", i=8))
+            k_rows = k[b].rearrange("(g p t) d -> g p t d", g=2, p=P, t=4)
+            q_rows = q[b].rearrange("(p i) d -> p i d", i=8)
+            for h in range(2):
+                nc.sync.dma_start(out=k_sb[b][:, 4 * h : 4 * h + 4, :], in_=k_rows[h])
+                nc.sync.dma_start(out=q_sb[b][:, 4 * h : 4 * h + 4, :], in_=q_rows[:, 4 * h : 4 * h + 4, :])
 
         def load_x(b):
             x_sb[b] = const.tile([P, 8 * F], BF16, name="x_sb%d" % b)
@@ -240,8 +240,8 @@ def tile_graphconvolution_wmask_learnadj_pa_t_kernel(tc, q, k, x, mask, weight, 
             out=w_raw[:].rearrange("w (u e) o -> w u e o", u=2),
             in_=weight.rearrange("(u w e) o -> w u e o", u=2, w=P, e=2),
         )
-        mask_sb = const.tile([P, NB, 8], BF16, name="mask_sb")
-        nc.sync.dma_start(out=mask_sb[:], in_=mask.rearrange("b (p i) -> p b i", i=8))
+        mask_sb = const.tile([P, NB * 8], BF16, name="mask_sb")
+        nc.sync.dma_start(out=mask_sb[:].rearrange("p (b i) -> p b i", i=8), in_=mask.rearrange("b (p i) -> p b i", i=8))
         for b in range(1, NB):
             load_qk(b)
             load_x(b)
@@ -249,11 +249,9 @@ def tile_graphconvolution_wmask_learnadj_pa_t_kernel(tc, q, k, x, mask, weight, 
         wg = const.tile([P, 4 * O], BF16, name="wg", align_bytes=64)
         wc = const.tile([P, O], U32, name="wc", align_bytes=64)
         ws = const.tile([P, O], U8, name="ws", align_bytes=64)
-        mask_f = const.tile([P, NB * 8], F32, name="mask_f")
 
-        qT, kT, xg, xc, xs, sg, sc, ss = {}, {}, {}, {}, {}, {}, {}, {}
+        kq, xg, xc, xs, sg, sc, ss = {}, {}, {}, {}, {}, {}, {}
         bank = {}
-        planes = {}
         sim, half_min, ns, nbias, rsum, e_sb, te, ge, ec, es, agg, scl = {}, {}, {}, {}, {}, {}, {}, {}, {}, {}, {}, {}
 
         def copy(eng, dst, src):
@@ -267,11 +265,13 @@ def tile_graphconvolution_wmask_learnadj_pa_t_kernel(tc, q, k, x, mask, weight, 
 
         def unit_tensor(unit, eng):
             kind, b = unit[0], unit[1]
-            if kind == "k" or kind == "q":
-                src = k_sb[b] if kind == "k" else q_sb[b]
+            if kind == "kq":
+                h = unit[2]
                 pt = rings[eng].tile([P, 8, P], BF16, name="bank" + eng, tag="bank" + eng)
-                for j in range(8):
-                    nc.tensor.transpose(pt[:, j, :], src[:, j, :], ident_bf[:])
+                for j in range(4):
+                    nc.tensor.transpose(pt[:, j, :], k_sb[b][:, 4 * h + j, :], ident_bf[:])
+                for j in range(4):
+                    nc.tensor.transpose(pt[:, 4 + j, :], q_sb[b][:, 4 * h + j, :], ident_bf[:])
             elif kind == "x":
                 words = x_sb[b][:].bitcast(F32)
                 pt = rings[eng].tile([P, 2, 2, P], F32, name="bank" + eng, tag="bank" + eng)
@@ -298,17 +298,21 @@ def tile_graphconvolution_wmask_learnadj_pa_t_kernel(tc, q, k, x, mask, weight, 
         def unit_finish(unit, eng):
             kind = unit[0]
             if kind == "wg":
-                copy(eng, wg[:].rearrange("w (o j) -> w o j", j=4), w_raw[:].rearrange("w j o -> w o j"))
+                nc.gpsimd.tensor_scalar(
+                    out=wg[:].rearrange("w (o j) -> w o j", j=4),
+                    in0=w_raw[:].rearrange("w j o -> w o j"),
+                    scalar1=1.0,
+                    scalar2=0.0,
+                    op0=ALU.mult,
+                    op1=ALU.add,
+                )
             elif kind == "Qw":
                 quantise(wc[:], ws[:], wg[:])
-            elif kind == "k" or kind == "q":
-                b = unit[1]
-                dst = graph.tile([P, N], BF16, name=kind + "T")
-                copy(eng, dst[:], bank[unit][:].rearrange("d j p -> d (j p)"))
-                if kind == "k":
-                    kT[b] = dst
-                else:
-                    qT[b] = dst
+            elif kind == "kq":
+                b, h = unit[1], unit[2]
+                if b not in kq:
+                    kq[b] = graph.tile([P, 2, N], BF16, name="kq")
+                copy(eng, kq[b][:, h, :], bank[unit][:].rearrange("d j p -> d (j p)"))
             elif kind == "x":
                 b, j = unit[1], unit[2]
                 if b not in xg:
@@ -337,8 +341,8 @@ def tile_graphconvolution_wmask_learnadj_pa_t_kernel(tc, q, k, x, mask, weight, 
             sim[(r, g)] = rings[eng].tile([P, 512], F32, name="bank" + eng, tag="bank" + eng)
             nc.tensor.matmul(
                 out=sim[(r, g)][:],
-                lhsT=qT[b][:, i * 128 : (i + 1) * 128],
-                rhs=kT[b][:, g * 512 : (g + 1) * 512],
+                lhsT=kq[b][:, i // 4, 512 + (i % 4) * 128 : 512 + (i % 4 + 1) * 128],
+                rhs=kq[b][:, g, 0:512],
                 start=True,
                 stop=True,
             )
@@ -377,19 +381,12 @@ def tile_graphconvolution_wmask_learnadj_pa_t_kernel(tc, q, k, x, mask, weight, 
                 nc.tensor.transpose(te[r][:, j, :], e_sb[r][:, j * 128 : (j + 1) * 128], ident_bf[:])
 
         def regroup(r, eng):
-            planes[r] = work.tile([P, N], BF16, name="planes")
-            copy(eng, planes[r][:], te[r][:].rearrange("p j n -> p (j n)"))
-
-        def interleave(r):
             if r % FG == 0:
                 ge[r // FG] = work.tile([P, FG * N], BF16, name="ge", align_bytes=64)
-            nc.gpsimd.tensor_scalar(
-                out=ge[r // FG][:, (r % FG) * N : (r % FG + 1) * N].rearrange("p (g n t) -> p g n t", g=2, n=P, t=4),
-                in0=planes[r][:].rearrange("p (g t n) -> p g n t", g=2, t=4),
-                scalar1=1.0,
-                scalar2=0.0,
-                op0=ALU.mult,
-                op1=ALU.add,
+            copy(
+                eng,
+                ge[r // FG][:, (r % FG) * N : (r % FG + 1) * N].rearrange("p (g n t) -> p g n t", g=2, n=P, t=4),
+                te[r][:].rearrange("p (g t) n -> p g n t", g=2, t=4),
             )
 
         def quantise_e(f):
@@ -413,12 +410,10 @@ def tile_graphconvolution_wmask_learnadj_pa_t_kernel(tc, q, k, x, mask, weight, 
                 )
 
         def row_scale(pair):
-            if pair == 0:
-                nc.vector.tensor_copy(out=mask_f[:], in_=mask_sb[:].rearrange("p b i -> p (b i)"))
             recip = small.tile([P, RG], F32, name="recip")
             nc.vector.reciprocal(out=recip[:], in_=rsum[pair][:])
             scl[pair] = late.tile([P, RG], F32, name="scl")
-            nc.vector.tensor_mul(out=scl[pair][:], in0=recip[:], in1=mask_f[:, RG * pair : RG * pair + RG])
+            nc.vector.tensor_mul(out=scl[pair][:], in0=recip[:], in1=mask_sb[:, RG * pair : RG * pair + RG])
 
         def way_out(r, eng):
             b, i = divmod(r, 8)
@@ -430,7 +425,7 @@ def tile_graphconvolution_wmask_learnadj_pa_t_kernel(tc, q, k, x, mask, weight, 
                 nc.scalar.activation(out=o_sb[:], in_=agg[r][:], func=AF.Copy, scale=factor)
             nc.sync.dma_start(out=out[b].rearrange("(p i) o -> p i o", i=8)[:, i, :], in_=o_sb[:])
 
-        for op in make_plan(V_BANKS, S_BANKS, (0, 1), (2,), (3, 3, 3), 40, 1, FG, RG):
+        for op in make_plan(V_BANKS, S_BANKS, (2, 2, 1), (1, 1, 0), (3, 2, 2), 40, 0, FG, RG):
             what, eng = op[0], op[-1]
             if what == "P":
                 unit_tensor(op[1:-1], eng)
@@ -446,8 +441,6 @@ def tile_graphconvolution_wmask_learnadj_pa_t_kernel(tc, q, k, x, mask, weight, 
                 flip(op[1], eng)
             elif what == "E":
                 regroup(op[1], eng)
-            elif what == "W":
-                interleave(op[1])
             elif what == "F":
                 quantise_e(op[1])
             elif what == "G":

@@ -225,21 +225,23 @@ def tile_graphconvolution_wmask_learnadj_pa_t_kernel(tc, q, k, x, mask, weight, 
                 nc.sync.dma_start(out=k_sb[b][:, 4 * h : 4 * h + 4, :], in_=k_rows[h])
                 nc.sync.dma_start(out=q_sb[b][:, 4 * h : 4 * h + 4, :], in_=q_rows[:, 4 * h : 4 * h + 4, :])
 
-        def load_x(b):
-            x_sb[b] = const.tile([P, 8 * F], BF16, name="x_sb%d" % b)
+        def load_x(b, halves=(0, 1)):
+            if b not in x_sb:
+                x_sb[b] = const.tile([P, 8 * F], BF16, name="x_sb%d" % b)
             rows = x[b].rearrange("(g p t) f -> g p t f", g=2, p=P, t=4)
-            for g in range(2):
+            for g in halves:
                 nc.sync.dma_start(
                     out=x_sb[b][:, g * 4 * F : (g + 1) * 4 * F].rearrange("p (t f) -> p t f", t=4), in_=rows[g]
                 )
 
         load_qk(0)
-        load_x(0)
+        load_x(0, (0,))
         w_raw = const.tile([P, 4, O], BF16, name="w_raw")
         nc.sync.dma_start(
             out=w_raw[:].rearrange("w (u e) o -> w u e o", u=2),
             in_=weight.rearrange("(u w e) o -> w u e o", u=2, w=P, e=2),
         )
+        load_x(0, (1,))
         mask_sb = const.tile([P, NB * 8], BF16, name="mask_sb")
         nc.sync.dma_start(out=mask_sb[:].rearrange("p (b i) -> p b i", i=8), in_=mask.rearrange("b (p i) -> p b i", i=8))
         for b in range(1, NB):
@@ -367,8 +369,8 @@ def tile_graphconvolution_wmask_learnadj_pa_t_kernel(tc, q, k, x, mask, weight, 
             if r % RG == 0:
                 rsum[r // RG] = small.tile([P, RG], F32, name="rsum")
             nc.scalar.activation(
-                out=e_sb[r][:],
-                in_=ns[r][:],
+                out=e_sb[r][:].rearrange("n (g p e) -> n g p e", g=4, e=2),
+                in_=ns[r][:].rearrange("n (g e p) -> n g p e", g=4, e=2),
                 func=AF.Exp,
                 bias=nbias[r][:, 0:1],
                 scale=-1.0,
@@ -376,17 +378,18 @@ def tile_graphconvolution_wmask_learnadj_pa_t_kernel(tc, q, k, x, mask, weight, 
             )
 
         def flip(r, eng):
-            te[r] = rings[eng].tile([P, 8, P], BF16, name="bank" + eng, tag="bank" + eng)
-            for j in range(8):
-                nc.tensor.transpose(te[r][:, j, :], e_sb[r][:, j * 128 : (j + 1) * 128], ident_bf[:])
+            te[r] = rings[eng].tile([P, 4, P], F32, name="bank" + eng, tag="bank" + eng)
+            words = e_sb[r][:].bitcast(F32)
+            for j in range(4):
+                nc.tensor.transpose(te[r][:, j, :], words[:, j * 128 : (j + 1) * 128], ident_f[:])
 
         def regroup(r, eng):
             if r % FG == 0:
                 ge[r // FG] = work.tile([P, FG * N], BF16, name="ge", align_bytes=64)
             copy(
                 eng,
-                ge[r // FG][:, (r % FG) * N : (r % FG + 1) * N].rearrange("p (g n t) -> p g n t", g=2, n=P, t=4),
-                te[r][:].rearrange("p (g t) n -> p g n t", g=2, t=4),
+                ge[r // FG][:, (r % FG) * N : (r % FG + 1) * N].bitcast(F32).rearrange("p (g n u) -> p g n u", g=2, n=P, u=2),
+                te[r][:].rearrange("p (g u) n -> p g n u", g=2, u=2),
             )
 
         def quantise_e(f):
@@ -425,7 +428,7 @@ def tile_graphconvolution_wmask_learnadj_pa_t_kernel(tc, q, k, x, mask, weight, 
                 nc.scalar.activation(out=o_sb[:], in_=agg[r][:], func=AF.Copy, scale=factor)
             nc.sync.dma_start(out=out[b].rearrange("(p i) o -> p i o", i=8)[:, i, :], in_=o_sb[:])
 
-        for op in make_plan(V_BANKS, S_BANKS, (2, 2, 1), (1, 1, 0), (3, 2, 2), 40, 0, FG, RG):
+        for op in make_plan(V_BANKS, S_BANKS, (1, 2), (1, 1, 2), (3, 2, 2), 40, 0, FG, RG):
             what, eng = op[0], op[-1]
             if what == "P":
                 unit_tensor(op[1:-1], eng)

@@ -18,10 +18,12 @@ P = 128
 FLOPS = 2 * NB * (N * N * D + N * F * O + N * N * O)
 V_BANKS = 5
 S_BANKS = 3
-FG = 2
+GROUPS = (4,) * 7 + (2, 1, 1)
 RG = 4
-LATE_BUFS = 10
+LATE_BUFS = 5
 
+GROUP_OF = [f for f in range(len(GROUPS)) for j in range(GROUPS[f])]
+GROUP_START = [sum(GROUPS[:f]) for f in range(len(GROUPS))]
 NT = 32
 IN_PSUM = ("x", "kq", "s")
 
@@ -50,7 +52,7 @@ def needs(unit):
     return []
 
 
-def step_lists(v_extra, s_extra, head, late, pool, fg, rg):
+def step_lists(v_extra, s_extra, head, rg):
     stream = stream_units()
     when = {("kq", 0, 0): -1, ("kq", 0, 1): -1}
     taken = set()
@@ -69,13 +71,13 @@ def step_lists(v_extra, s_extra, head, late, pool, fg, rg):
 
     def tile_for(s):
         r = st["tile"]
-        if r < NT and f_step.get(r // fg, s) < s and r_step.get(r // rg, s) < s and when.get(("Qs", r // 8), s) < s:
+        if r < NT and f_step.get(GROUP_OF[r], s) < s and r_step.get(r // rg, s) < s and when.get(("Qs", r // 8), s) < s:
             return r
         return None
 
-    def extra(s, tiles_first):
+    def extra(s):
         unit, r = unit_for(s), tile_for(s)
-        if r is not None and (tiles_first or unit is None):
+        if r is not None:
             st["tile"] += 1
             return ("H", r)
         if unit is not None:
@@ -91,29 +93,29 @@ def step_lists(v_extra, s_extra, head, late, pool, fg, rg):
             v += [("B", s, 0), ("B", s, 1)]
         if 0 <= s - 1 < NT:
             sc.append(("C", s - 1))
-        n_s = head[s] if s < len(head) else (0 if late <= s < NT else s_extra[s % len(s_extra)])
-        for rep in range(n_s):
-            item = extra(s, True)
-            if item is not None:
-                sc.append(item)
+        if 0 <= s - 2 < NT:
+            sc.append(("E", s - 2))
         if s == 0:
             taken.add(("wg",))
             when[("wg",)] = s
             sc.append(("U", "wg"))
-        if 0 <= s - 2 < NT:
-            if pool:
-                v.append(("E", s - 2))
-                v.append(("W", s - 2))
-            else:
-                sc.append(("E", s - 2))
-        for rep in range(0 if s == 0 else (3 if s >= late else v_extra[s % len(v_extra)])):
-            item = extra(s, False)
-            if item is not None:
-                v.append(item)
-        r = s - 3 - pool
-        if 0 <= r < NT and r % fg == fg - 1:
-            v.append(("F", r // fg))
-            f_step[r // fg] = s
+        n_s = head[s] if s < len(head) else s_extra[s % len(s_extra)]
+        n_v = 0 if s == 0 else v_extra[s % len(v_extra)]
+        if s > NT:
+            n_v, n_s = 2, 2
+        for rep in range(max(n_s, n_v)):
+            if rep < n_s:
+                item = extra(s)
+                if item is not None:
+                    sc.append(item)
+            if rep < n_v:
+                item = extra(s)
+                if item is not None:
+                    v.append(item)
+        r = s - 3
+        if 0 <= r < NT and (r == NT - 1 or GROUP_OF[r + 1] != GROUP_OF[r]):
+            v.append(("F", GROUP_OF[r]))
+            f_step[GROUP_OF[r]] = s
         r = s - 2
         if 0 <= r < NT and r % rg == rg - 1:
             v.append(("R", r // rg))
@@ -144,8 +146,8 @@ def fill_of(op):
     return None
 
 
-def make_plan(v_banks, s_banks, v_extra, s_extra, head, late, pool, fg, rg):
-    steps = [([("U", "kq", 0, 0)], [("U", "kq", 0, 1)])] + step_lists(v_extra, s_extra, head, late, pool, fg, rg)
+def make_plan(v_banks, s_banks, v_extra, s_extra, head, rg):
+    steps = [([("U", "kq", 0, 0)], [("U", "kq", 0, 1)])] + step_lists(v_extra, s_extra, head, rg)
 
     def fill_needs(fill):
         if fill[0] == "A":
@@ -153,7 +155,7 @@ def make_plan(v_banks, s_banks, v_extra, s_extra, head, late, pool, fg, rg):
         if fill[0] == "T":
             return [("C", fill[1])]
         if fill[0] == "G":
-            return [("F", fill[1] // fg), ("U", "Qs", fill[1] // 8)]
+            return [("F", GROUP_OF[fill[1]]), ("U", "Qs", fill[1] // 8)]
         return [("U",) + d for d in needs(fill[1:])]
 
     rings = {}
@@ -167,7 +169,7 @@ def make_plan(v_banks, s_banks, v_extra, s_extra, head, late, pool, fg, rg):
         progress = True
         while progress:
             progress = False
-            for eng in ("S", "V"):
+            for eng in ("V", "S"):
                 ring = rings[eng]
                 if ring["filled"] < len(ring["fills"]) and ring["filled"] - ring["emptied"] < ring["banks"]:
                     fill = ring["fills"][ring["filled"]]
@@ -384,28 +386,31 @@ def tile_graphconvolution_wmask_learnadj_pa_t_kernel(tc, q, k, x, mask, weight, 
                 nc.tensor.transpose(te[r][:, j, :], words[:, j * 128 : (j + 1) * 128], ident_f[:])
 
         def regroup(r, eng):
-            if r % FG == 0:
-                ge[r // FG] = work.tile([P, FG * N], BF16, name="ge", align_bytes=64)
+            f = GROUP_OF[r]
+            i = r - GROUP_START[f]
+            if i == 0:
+                ge[f] = work.tile([P, GROUPS[f] * N], BF16, name="ge", align_bytes=64)
             copy(
                 eng,
-                ge[r // FG][:, (r % FG) * N : (r % FG + 1) * N].bitcast(F32).rearrange("p (g n u) -> p g n u", g=2, n=P, u=2),
+                ge[f][:, i * N : (i + 1) * N].bitcast(F32).rearrange("p (g n u) -> p g n u", g=2, n=P, u=2),
                 te[r][:].rearrange("p (g u) n -> p g n u", g=2, u=2),
             )
 
         def quantise_e(f):
-            ec[f] = late.tile([P, FG * 256], U32, name="ec", align_bytes=64)
-            es[f] = late.tile([P, FG * 256], U8, name="es", align_bytes=64)
+            ec[f] = late.tile([P, GROUPS[f] * 256], U32, name="ec", align_bytes=64)
+            es[f] = late.tile([P, GROUPS[f] * 256], U8, name="es", align_bytes=64)
             quantise(ec[f][:], es[f][:], ge[f][:])
 
         def aggregate(r, eng):
             b = r // 8
+            f = GROUP_OF[r]
             agg[r] = rings[eng].tile([P, O], F32, name="bank" + eng, tag="bank" + eng)
             for g in range(2):
-                n0 = (r % FG) * 256 + g * 128
+                n0 = (r - GROUP_START[f]) * 256 + g * 128
                 nc.tensor.matmul_mx(
                     out=agg[r][:],
-                    lhsT=ec[r // FG][:, n0 : n0 + 128].bitcast(FP8X4),
-                    lhsT_scale=es[r // FG][:, n0 : n0 + 128],
+                    lhsT=ec[f][:, n0 : n0 + 128].bitcast(FP8X4),
+                    lhsT_scale=es[f][:, n0 : n0 + 128],
                     rhs=sc[b][:, g * O : (g + 1) * O].bitcast(FP8X4),
                     rhs_scale=ss[b][:, g * O : (g + 1) * O],
                     start=(g == 0),
@@ -428,7 +433,7 @@ def tile_graphconvolution_wmask_learnadj_pa_t_kernel(tc, q, k, x, mask, weight, 
                 nc.scalar.activation(out=o_sb[:], in_=agg[r][:], func=AF.Copy, scale=factor)
             nc.sync.dma_start(out=out[b].rearrange("(p i) o -> p i o", i=8)[:, i, :], in_=o_sb[:])
 
-        for op in make_plan(V_BANKS, S_BANKS, (1, 2), (1, 1, 2), (3, 2, 2), 40, 0, FG, RG):
+        def emit(op):
             what, eng = op[0], op[-1]
             if what == "P":
                 unit_tensor(op[1:-1], eng)
@@ -452,3 +457,11 @@ def tile_graphconvolution_wmask_learnadj_pa_t_kernel(tc, q, k, x, mask, weight, 
                 row_scale(op[1])
             else:
                 way_out(op[1], eng)
+
+        plan = make_plan(V_BANKS, S_BANKS, (1, 1, 2), (2, 1, 2), (3, 2, 2), RG)
+        first = 1 + plan.index(("U", "Qw", "V"))
+        with tc.manual_schedule(engines={mybir.EngineType.DVE}):
+            for op in plan[:first]:
+                emit(op)
+        for op in plan[first:]:
+            emit(op)

@@ -89,8 +89,12 @@ def step_lists(v_extra, s_extra, head, rg):
     s = 0
     while st["tile"] < NT:
         v, sc = [], []
+        if s == 0:
+            v.append(("B", 0, 0))
+        if s + 1 < NT:
+            v.append(("B", s + 1, 0))
         if s < NT:
-            v += [("B", s, 0), ("B", s, 1)]
+            v.append(("B", s, 1))
         if 0 <= s - 1 < NT:
             sc.append(("C", s - 1))
         if 0 <= s - 2 < NT:

@@ -20,7 +20,7 @@ V_BANKS = 5
 S_BANKS = 3
 GROUPS = (4,) * 7 + (2, 1, 1)
 RG = 4
-LATE_BUFS = 5
+LATE_BUFS = 6
 
 GROUP_OF = [f for f in range(len(GROUPS)) for j in range(GROUPS[f])]
 GROUP_START = [sum(GROUPS[:f]) for f in range(len(GROUPS))]
@@ -52,7 +52,7 @@ def needs(unit):
     return []
 
 
-def step_lists(v_extra, s_extra, head, rg):
+def step_lists(v_extra, s_extra, head, rg, backlog, e_on_v):
     stream = stream_units()
     when = {("kq", 0, 0): -1, ("kq", 0, 1): -1}
     taken = set()
@@ -64,9 +64,8 @@ def step_lists(v_extra, s_extra, head, rg):
     def unit_for(s):
         for unit in stream:
             if unit[0] in IN_PSUM and unit not in taken:
-                if all(when.get(d, s) < s for d in needs(unit)):
+                if all(when.get(d, s) < s for d in needs(unit)) and (unit[0] != "kq" or s > 8 * (unit[1] - 1)):
                     return unit
-                return None
         return None
 
     def tile_for(s):
@@ -77,7 +76,7 @@ def step_lists(v_extra, s_extra, head, rg):
 
     def extra(s):
         unit, r = unit_for(s), tile_for(s)
-        if r is not None:
+        if r is not None and (unit is None or sum(GROUPS[f] for f in f_step) - r > backlog):
             st["tile"] += 1
             return ("H", r)
         if unit is not None:
@@ -98,7 +97,7 @@ def step_lists(v_extra, s_extra, head, rg):
         if 0 <= s - 1 < NT:
             sc.append(("C", s - 1))
         if 0 <= s - 2 < NT:
-            sc.append(("E", s - 2))
+            (v if s - 2 >= e_on_v else sc).append(("E", s - 2))
         if s == 0:
             taken.add(("wg",))
             when[("wg",)] = s
@@ -130,8 +129,6 @@ def step_lists(v_extra, s_extra, head, rg):
                     taken.add(unit)
                     when[unit] = s
                     v.append(("U",) + unit)
-                else:
-                    break
         steps.append((v, sc))
         s += 1
         assert s < 70
@@ -150,8 +147,8 @@ def fill_of(op):
     return None
 
 
-def make_plan(v_banks, s_banks, v_extra, s_extra, head, rg):
-    steps = [([("U", "kq", 0, 0)], [("U", "kq", 0, 1)])] + step_lists(v_extra, s_extra, head, rg)
+def make_plan(v_banks, s_banks, v_extra, s_extra, head, rg, backlog, e_on_v):
+    steps = [([("U", "kq", 0, 0)], [("U", "kq", 0, 1)])] + step_lists(v_extra, s_extra, head, rg, backlog, e_on_v)
 
     def fill_needs(fill):
         if fill[0] == "A":
@@ -219,6 +216,9 @@ def tile_graphconvolution_wmask_learnadj_pa_t_kernel(tc, q, k, x, mask, weight, 
         make_identity(nc, ident_bf[:])
         ident_f = const.tile([P, P], F32, name="ident_f")
         make_identity(nc, ident_f[:])
+
+        minus_one = const.tile([P, RG], F32, name="minus_one")
+        nc.gpsimd.memset(minus_one[:], -1.0)
 
         k_sb, q_sb, x_sb = {}, {}, {}
 
@@ -423,9 +423,9 @@ def tile_graphconvolution_wmask_learnadj_pa_t_kernel(tc, q, k, x, mask, weight, 
 
         def row_scale(pair):
             recip = small.tile([P, RG], F32, name="recip")
-            nc.vector.reciprocal(out=recip[:], in_=rsum[pair][:])
+            nc.gpsimd.tensor_tensor(out=recip[:], in0=rsum[pair][:], in1=minus_one[:], op=ALU.pow)
             scl[pair] = late.tile([P, RG], F32, name="scl")
-            nc.vector.tensor_mul(out=scl[pair][:], in0=recip[:], in1=mask_sb[:, RG * pair : RG * pair + RG])
+            nc.gpsimd.tensor_mul(out=scl[pair][:], in0=recip[:], in1=mask_sb[:, RG * pair : RG * pair + RG])
 
         def way_out(r, eng):
             b, i = divmod(r, 8)
@@ -462,7 +462,7 @@ def tile_graphconvolution_wmask_learnadj_pa_t_kernel(tc, q, k, x, mask, weight, 
             else:
                 way_out(op[1], eng)
 
-        plan = make_plan(V_BANKS, S_BANKS, (1, 1, 2), (2, 1, 2), (3, 2, 2), RG)
+        plan = make_plan(V_BANKS, S_BANKS, (1,), (1, 1, 2), (3, 2, 2), RG, 9, 28)
         first = 1 + plan.index(("U", "Qw", "V"))
         with tc.manual_schedule(engines={mybir.EngineType.DVE}):
             for op in plan[:first]:

from contextlib import ExitStack
import math

import concourse.mybir as mybir
from concourse.masks import make_identity

FP8X4 = mybir.dt.float8_e4m3fn_x4
BF16 = mybir.dt.bfloat16
F32 = mybir.dt.float32
U32 = mybir.dt.uint32
U8 = mybir.dt.uint8
AF = mybir.ActivationFunctionType
ALU = mybir.AluOpType
AX = mybir.AxisListType

NB, N, F, D, O = 4, 1024, 512, 128, 512
P = 128
FLOPS = 2 * NB * (N * N * D + N * F * O + N * N * O)
V_BANKS = 5
S_BANKS = 3
GROUPS = (4,) * 7 + (2, 1, 1)
RG = 4
LATE_BUFS = 6

GROUP_OF = [f for f in range(len(GROUPS)) for j in range(GROUPS[f])]
GROUP_START = [sum(GROUPS[:f]) for f in range(len(GROUPS))]
NT = 32
IN_PSUM = ("x", "kq", "s")


def stream_units():
    units = [("wg",), ("Qw",)]
    for b in range(4):
        units += [("x", b, j) for j in range(4)]
        if b < 3:
            units += [("kq", b + 1, 0), ("kq", b + 1, 1)]
        units += [("Qx", b)]
        units += [("s", b, g, c) for g in range(2) for c in range(4)]
        units += [("Qs", b)]
    return units


def needs(unit):
    if unit[0] == "s":
        return [("Qx", unit[1]), ("Qw",)]
    if unit[0] == "Qw":
        return [("wg",)]
    if unit[0] == "Qx":
        return [("x", unit[1], j) for j in range(4)]
    if unit[0] == "Qs":
        return [("s", unit[1], g, c) for g in range(2) for c in range(4)]
    return []


def step_lists(v_extra, s_extra, head, rg, backlog, e_on_v):
    stream = stream_units()
    when = {("kq", 0, 0): -1, ("kq", 0, 1): -1}
    taken = set()
    st = {"tile": 0}
    f_step = {}
    r_step = {}
    steps = []

    def unit_for(s):
        for unit in stream:
            if unit[0] in IN_PSUM and unit not in taken:
                if all(when.get(d, s) < s for d in needs(unit)) and (unit[0] != "kq" or s > 8 * (unit[1] - 1)):
                    return unit
        return None

    def tile_for(s):
        r = st["tile"]
        if r < NT and f_step.get(GROUP_OF[r], s) < s and r_step.get(r // rg, s) < s and when.get(("Qs", r // 8), s) < s:
            return r
        return None

    def extra(s):
        unit, r = unit_for(s), tile_for(s)
        if r is not None and (unit is None or sum(GROUPS[f] for f in f_step) - r > backlog):
            st["tile"] += 1
            return ("H", r)
        if unit is not None:
            taken.add(unit)
            when[unit] = s
            return ("U",) + unit
        return None

    s = 0
    while st["tile"] < NT:
        v, sc = [], []
        if s == 0:
            v.append(("B", 0, 0))
        if s + 1 < NT:
            v.append(("B", s + 1, 0))
        if s < NT:
            v.append(("B", s, 1))
        if 0 <= s - 1 < NT:
            sc.append(("C", s - 1))
        if 0 <= s - 2 < NT:
            (v if s - 2 >= e_on_v else sc).append(("E", s - 2))
        if s == 0:
            taken.add(("wg",))
            when[("wg",)] = s
            sc.append(("U", "wg"))
        n_s = head[s] if s < len(head) else s_extra[s % len(s_extra)]
        n_v = 0 if s == 0 else v_extra[s % len(v_extra)]
        if s > NT:
            n_v, n_s = 2, 2
        for rep in range(max(n_s, n_v)):
            if rep < n_s:
                item = extra(s)
                if item is not None:
                    sc.append(item)
            if rep < n_v:
                item = extra(s)
                if item is not None:
                    v.append(item)
        r = s - 3
        if 0 <= r < NT and (r == NT - 1 or GROUP_OF[r + 1] != GROUP_OF[r]):
            v.append(("F", GROUP_OF[r]))
            f_step[GROUP_OF[r]] = s
        r = s - 2
        if 0 <= r < NT and r % rg == rg - 1:
            v.append(("R", r // rg))
            r_step[r // rg] = s
        for unit in stream:
            if unit[0] not in IN_PSUM and unit not in taken:
                if all(when.get(d, s) < s or ("U",) + d in v for d in needs(unit)):
                    taken.add(unit)
                    when[unit] = s
                    v.append(("U",) + unit)
        steps.append((v, sc))
        s += 1
        assert s < 70
    return steps


def fill_of(op):
    if op[0] == "B":
        return ("A", op[1], op[2])
    if op[0] == "E":
        return ("T", op[1])
    if op[0] == "H":
        return ("G", op[1])
    if op[0] == "U" and op[1] in IN_PSUM:
        return ("P",) + op[1:]
    return None


def make_plan(v_banks, s_banks, v_extra, s_extra, head, rg, backlog, e_on_v):
    steps = [([("U", "kq", 0, 0)], [("U", "kq", 0, 1)])] + step_lists(v_extra, s_extra, head, rg, backlog, e_on_v)

    def fill_needs(fill):
        if fill[0] == "A":
            return [("U", "kq", fill[1] // 8, fill[2]), ("U", "kq", fill[1] // 8, (fill[1] % 8) // 4)]
        if fill[0] == "T":
            return [("C", fill[1])]
        if fill[0] == "G":
            return [("F", GROUP_OF[fill[1]]), ("U", "Qs", fill[1] // 8)]
        return [("U",) + d for d in needs(fill[1:])]

    rings = {}
    for eng, idx, banks in (("V", 0, v_banks), ("S", 1, s_banks)):
        fills = [fill_of(op) for step in steps for op in step[idx] if fill_of(op) is not None]
        rings[eng] = {"fills": fills, "banks": banks, "filled": 0, "emptied": 0}
    ops = []
    written = set()

    def top_up():
        progress = True
        while progress:
            progress = False
            for eng in ("V", "S"):
                ring = rings[eng]
                if ring["filled"] < len(ring["fills"]) and ring["filled"] - ring["emptied"] < ring["banks"]:
                    fill = ring["fills"][ring["filled"]]
                    if all(d in written for d in fill_needs(fill)):
                        ops.append(fill + (eng,))
                        ring["filled"] += 1
                        progress = True

    def write(op, eng):
        if fill_of(op) is not None:
            assert rings[eng]["emptied"] < rings[eng]["filled"], op
            rings[eng]["emptied"] += 1
        ops.append(op + (eng,))
        written.add(op)
        top_up()

    top_up()
    for v, sc in steps:
        for i in range(max(len(v), len(sc))):
            if i < len(v):
                write(v[i], "G" if v[i][0] == "W" else "V")
            if i < len(sc):
                write(sc[i], "G" if sc[i] == ("U", "wg") else "S")
    return ops


def tile_graphconvolution_wmask_learnadj_pa_t_kernel(tc, q, k, x, mask, weight, out):
    nc = tc.nc
    scale = 1.0 / math.sqrt(D)
    with ExitStack() as ctx:
        const = ctx.enter_context(tc.tile_pool(name="const", bufs=1))
        graph = ctx.enter_context(tc.tile_pool(name="graph", bufs=2))
        graph3 = ctx.enter_context(tc.tile_pool(name="graph3", bufs=3))
        work = ctx.enter_context(tc.tile_pool(name="work", bufs=3))
        small = ctx.enter_context(tc.tile_pool(name="small", bufs=4))
        late = ctx.enter_context(tc.tile_pool(name="late", bufs=LATE_BUFS))
        outs = ctx.enter_context(tc.tile_pool(name="outs", bufs=12))
        ring_v = ctx.enter_context(tc.psum_pool(name="ring_v", bufs=V_BANKS))
        ring_s = ctx.enter_context(tc.psum_pool(name="ring_s", bufs=S_BANKS))
        rings = {"V": ring_v, "S": ring_s}

        ident_bf = const.tile([P, P], BF16, name="ident_bf")
        make_identity(nc, ident_bf[:])
        ident_f = const.tile([P, P], F32, name="ident_f")
        make_identity(nc, ident_f[:])

        minus_one = const.tile([P, RG], F32, name="minus_one")
        nc.gpsimd.memset(minus_one[:], -1.0)

        k_sb, q_sb, x_sb = {}, {}, {}

        def load_qk(b):
            k_sb[b] = const.tile([P, 8, D], BF16, name="k_sb%d" % b)
            q_sb[b] = const.tile([P, 8, D], BF16, name="q_sb%d" % b)
            k_rows = k[b].rearrange("(g p t) d -> g p t d", g=2, p=P, t=4)
            q_rows = q[b].rearrange("(p i) d -> p i d", i=8)
            for h in range(2):
                nc.sync.dma_start(out=k_sb[b][:, 4 * h : 4 * h + 4, :], in_=k_rows[h])
                nc.sync.dma_start(out=q_sb[b][:, 4 * h : 4 * h + 4, :], in_=q_rows[:, 4 * h : 4 * h + 4, :])

        def load_x(b, halves=(0, 1)):
            if b not in x_sb:
                x_sb[b] = const.tile([P, 8 * F], BF16, name="x_sb%d" % b)
            rows = x[b].rearrange("(g p t) f -> g p t f", g=2, p=P, t=4)
            for g in halves:
                nc.sync.dma_start(
                    out=x_sb[b][:, g * 4 * F : (g + 1) * 4 * F].rearrange("p (t f) -> p t f", t=4), in_=rows[g]
                )

        load_qk(0)
        load_x(0, (0,))
        w_raw = const.tile([P, 4, O], BF16, name="w_raw")
        nc.sync.dma_start(
            out=w_raw[:].rearrange("w (u e) o -> w u e o", u=2),
            in_=weight.rearrange("(u w e) o -> w u e o", u=2, w=P, e=2),
        )
        load_x(0, (1,))
        mask_sb = const.tile([P, NB * 8], BF16, name="mask_sb")
        nc.sync.dma_start(out=mask_sb[:].rearrange("p (b i) -> p b i", i=8), in_=mask.rearrange("b (p i) -> p b i", i=8))
        for b in range(1, NB):
            load_qk(b)
            load_x(b)

        wg = const.tile([P, 4 * O], BF16, name="wg", align_bytes=64)
        wc = const.tile([P, O], U32, name="wc", align_bytes=64)
        ws = const.tile([P, O], U8, name="ws", align_bytes=64)

        kq, xg, xc, xs, sg, sc, ss = {}, {}, {}, {}, {}, {}, {}
        bank = {}
        sim, half_min, ns, nbias, rsum, e_sb, te, ge, ec, es, agg, scl = {}, {}, {}, {}, {}, {}, {}, {}, {}, {}, {}, {}

        def copy(eng, dst, src):
            if eng == "V":
                nc.vector.tensor_copy(out=dst, in_=src)
            else:
                nc.scalar.copy(out=dst, in_=src)

        def quantise(codes, scales, values):
            nc.vector.quantize_mx(out=codes.bitcast(FP8X4), scales=scales, in_=values)

        def unit_tensor(unit, eng):
            kind, b = unit[0], unit[1]
            if kind == "kq":
                h = unit[2]
                pt = rings[eng].tile([P, 8, P], BF16, name="bank" + eng, tag="bank" + eng)
                for j in range(4):
                    nc.tensor.transpose(pt[:, j, :], k_sb[b][:, 4 * h + j, :], ident_bf[:])
                for j in range(4):
                    nc.tensor.transpose(pt[:, 4 + j, :], q_sb[b][:, 4 * h + j, :], ident_bf[:])
            elif kind == "x":
                words = x_sb[b][:].bitcast(F32)
                pt = rings[eng].tile([P, 2, 2, P], F32, name="bank" + eng, tag="bank" + eng)
                for a in range(2):
                    for u in range(2):
                        c0 = (2 * unit[2] + a) * 256 + u * 128
                        nc.tensor.transpose(pt[:, a, u, :], words[:, c0 : c0 + 128], ident_f[:])
            else:
                g, c = unit[2], unit[3]
                pt = rings[eng].tile([P, 4, P], F32, name="bank" + eng, tag="bank" + eng)
                for t in range(4):
                    m0 = (4 * g + t) * 128
                    nc.tensor.matmul_mx(
                        out=pt[:, t, :],
                        lhsT=xc[b][:, m0 : m0 + 128].bitcast(FP8X4),
                        lhsT_scale=xs[b][:, m0 : m0 + 128],
                        rhs=wc[:, c * 128 : (c + 1) * 128].bitcast(FP8X4),
                        rhs_scale=ws[:, c * 128 : (c + 1) * 128],
                        start=True,
                        stop=True,
                    )
            bank[unit] = pt

        def unit_finish(unit, eng):
            kind = unit[0]
            if kind == "wg":
                nc.gpsimd.tensor_scalar(
                    out=wg[:].rearrange("w (o j) -> w o j", j=4),
                    in0=w_raw[:].rearrange("w j o -> w o j"),
                    scalar1=1.0,
                    scalar2=0.0,
                    op0=ALU.mult,
                    op1=ALU.add,
                )
            elif kind == "Qw":
                quantise(wc[:], ws[:], wg[:])
            elif kind == "kq":
                b, h = unit[1], unit[2]
                if b not in kq:
                    kq[b] = graph.tile([P, 2, N], BF16, name="kq")
                copy(eng, kq[b][:, h, :], bank[unit][:].rearrange("d j p -> d (j p)"))
            elif kind == "x":
                b, j = unit[1], unit[2]
                if b not in xg:
                    xg[b] = graph.tile([P, 8 * 512], BF16, name="xg", align_bytes=64)
                view = xg[b][:].bitcast(F32).rearrange("w (a p u) -> w a p u", a=8, p=P, u=2)
                copy(eng, view[:, 2 * j : 2 * j + 2, :, :], bank[unit][:].rearrange("w a u p -> w a p u"))
            elif kind == "Qx":
                b = unit[1]
                xc[b] = graph.tile([P, 1024], U32, name="xc", align_bytes=64)
                xs[b] = graph.tile([P, 1024], U8, name="xs", align_bytes=64)
                quantise(xc[b][:], xs[b][:], xg[b][:])
            elif kind == "s":
                b, g, c = unit[1], unit[2], unit[3]
                if b not in sg:
                    sg[b] = graph.tile([P, 2 * 4 * O], BF16, name="sg", align_bytes=64)
                view = sg[b][:].rearrange("p (g o t) -> p g o t", g=2, o=O, t=4)
                copy(eng, view[:, g, c * 128 : (c + 1) * 128, :], bank[unit][:].rearrange("p t o -> p o t"))
            else:
                b = unit[1]
                sc[b] = graph3.tile([P, 2 * O], U32, name="sc", align_bytes=64)
                ss[b] = graph3.tile([P, 2 * O], U8, name="ss", align_bytes=64)
                quantise(sc[b][:], ss[b][:], sg[b][:])

        def similarity(r, g, eng):
            b, i = divmod(r, 8)
            sim[(r, g)] = rings[eng].tile([P, 512], F32, name="bank" + eng, tag="bank" + eng)
            nc.tensor.matmul(
                out=sim[(r, g)][:],
                lhsT=kq[b][:, i // 4, 512 + (i % 4) * 128 : 512 + (i % 4 + 1) * 128],
                rhs=kq[b][:, g, 0:512],
                start=True,
                stop=True,
            )

        def row_max(r, g):
            if g == 0:
                ns[r] = work.tile([P, N], F32, name="ns", bufs=4)
                half_min[r] = small.tile([P, 1], F32, name="half_min")
                nbias[r] = small.tile([P, 1], F32, name="nbias")
            nc.vector.tensor_scalar(
                out=ns[r][:, g * 512 : (g + 1) * 512],
                in0=sim[(r, g)][:],
                scalar1=-scale,
                scalar2=None if g == 0 else half_min[r][:, 0:1],
                op0=ALU.mult,
                op1=ALU.min,
                accum_out=half_min[r][:, 0:1] if g == 0 else nbias[r][:, 0:1],
            )

        def exponential(r):
            e_sb[r] = work.tile([P, N], BF16, name="e_sb")
            if r % RG == 0:
                rsum[r // RG] = small.tile([P, RG], F32, name="rsum")
            nc.scalar.activation(
                out=e_sb[r][:].rearrange("n (g p e) -> n g p e", g=4, e=2),
                in_=ns[r][:].rearrange("n (g e p) -> n g p e", g=4, e=2),
                func=AF.Exp,
                bias=nbias[r][:, 0:1],
                scale=-1.0,
                accum_out=rsum[r // RG][:, r % RG : r % RG + 1],
            )

        def flip(r, eng):
            te[r] = rings[eng].tile([P, 4, P], F32, name="bank" + eng, tag="bank" + eng)
            words = e_sb[r][:].bitcast(F32)
            for j in range(4):
                nc.tensor.transpose(te[r][:, j, :], words[:, j * 128 : (j + 1) * 128], ident_f[:])

        def regroup(r, eng):
            f = GROUP_OF[r]
            i = r - GROUP_START[f]
            if i == 0:
                ge[f] = work.tile([P, GROUPS[f] * N], BF16, name="ge", align_bytes=64)
            copy(
                eng,
                ge[f][:, i * N : (i + 1) * N].bitcast(F32).rearrange("p (g n u) -> p g n u", g=2, n=P, u=2),
                te[r][:].rearrange("p (g u) n -> p g n u", g=2, u=2),
            )

        def quantise_e(f):
            ec[f] = late.tile([P, GROUPS[f] * 256], U32, name="ec", align_bytes=64)
            es[f] = late.tile([P, GROUPS[f] * 256], U8, name="es", align_bytes=64)
            quantise(ec[f][:], es[f][:], ge[f][:])

        def aggregate(r, eng):
            b = r // 8
            f = GROUP_OF[r]
            agg[r] = rings[eng].tile([P, O], F32, name="bank" + eng, tag="bank" + eng)
            for g in range(2):
                n0 = (r - GROUP_START[f]) * 256 + g * 128
                nc.tensor.matmul_mx(
                    out=agg[r][:],
                    lhsT=ec[f][:, n0 : n0 + 128].bitcast(FP8X4),
                    lhsT_scale=es[f][:, n0 : n0 + 128],
                    rhs=sc[b][:, g * O : (g + 1) * O].bitcast(FP8X4),
                    rhs_scale=ss[b][:, g * O : (g + 1) * O],
                    start=(g == 0),
                    stop=(g == 1),
                )

        def row_scale(pair):
            recip = small.tile([P, RG], F32, name="recip")
            nc.gpsimd.tensor_tensor(out=recip[:], in0=rsum[pair][:], in1=minus_one[:], op=ALU.pow)
            scl[pair] = late.tile([P, RG], F32, name="scl")
            nc.gpsimd.tensor_mul(out=scl[pair][:], in0=recip[:], in1=mask_sb[:, RG * pair : RG * pair + RG])

        def way_out(r, eng):
            b, i = divmod(r, 8)
            o_sb = outs.tile([P, O], F32, name="o_sb")
            factor = scl[r // RG][:, r % RG : r % RG + 1]
            if eng == "V":
                nc.vector.tensor_scalar(out=o_sb[:], in0=agg[r][:], scalar1=factor, scalar2=None, op0=ALU.mult)
            else:
                nc.scalar.activation(out=o_sb[:], in_=agg[r][:], func=AF.Copy, scale=factor)
            nc.sync.dma_start(out=out[b].rearrange("(p i) o -> p i o", i=8)[:, i, :], in_=o_sb[:])

        def emit(op):
            what, eng = op[0], op[-1]
            if what == "P":
                unit_tensor(op[1:-1], eng)
            elif what == "U":
                unit_finish(op[1:-1], eng)
            elif what == "A":
                similarity(op[1], op[2], eng)
            elif what == "B":
                row_max(op[1], op[2])
            elif what == "C":
                exponential(op[1])
            elif what == "T":
                flip(op[1], eng)
            elif what == "E":
                regroup(op[1], eng)
            elif what == "F":
                quantise_e(op[1])
            elif what == "G":
                aggregate(op[1], eng)
            elif what == "R":
                row_scale(op[1])
            else:
                way_out(op[1], eng)

        plan = make_plan(V_BANKS, S_BANKS, (1,), (1, 1, 2), (3, 2, 2), RG, 9, 28)
        first = 1 + plan.index(("U", "Qw", "V"))
        with tc.manual_schedule(engines={mybir.EngineType.DVE}):
            for op in plan[:first]:
                emit(op)
        for op in plan[first:]:
            emit(op)
